import numpy as np
import ml_dtypes


def mxq(x, axis, fmt="e4m3"):
    dtype, down = {"e4m3": (ml_dtypes.float8_e4m3fn, 7), "e5m2": (ml_dtypes.float8_e5m2, 14)}[fmt]
    v = np.moveaxis(np.asarray(x, np.float32).astype(ml_dtypes.bfloat16).astype(np.float64), axis, -1)
    blocks = v.reshape(v.shape[:-1] + (-1, 32))
    amax = np.abs(blocks).max(-1, keepdims=True)
    byte = np.maximum(np.where(amax > 0, np.frexp(amax)[1] - 1 + 127, 0) - down, 1)
    scale = np.exp2(byte - 127.0)
    codes = (blocks / scale).astype(np.float32).astype(dtype).astype(np.float64)
    return np.moveaxis((codes * scale).reshape(v.shape), -1, axis)


WIDE = False


def mx_kscale(k):
    if not WIDE:
        return np.ones(k)
    levels = np.array([10, -10, 5, -5, 0])
    a = np.random.permutation(np.resize(levels, k // 512 * 4)).reshape(k // 512, 4)
    idx = np.arange(k)
    return np.exp2(a[idx // 512, idx % 128 // 32])


BF16 = ml_dtypes.bfloat16


def bf(x):
    return np.asarray(x, np.float32).astype(BF16)


def f64(x):
    return np.asarray(x).astype(np.float64)


N, BI, BJ, C = 512, 64, 128, 128
EPS = 1e-5


def layernorm(v, w, b):
    mu = v.mean(-1, keepdims=True)
    var = np.square(v - mu).mean(-1, keepdims=True)
    return (v - mu) * (1.0 / np.sqrt(var + EPS)) * w + b


def setup_inputs():
    s = mx_kscale(N)[None, :, None]
    return {"a_proj": bf(np.random.standard_normal((BI, N, C)) * 0.5 * s),
            "b_proj": bf(np.random.standard_normal((BJ, N, C)) * 0.5 / s),
            "ln2_w": bf(1.0 + 0.1 * np.random.standard_normal(C)),
            "ln2_b": bf(0.1 * np.random.standard_normal(C))}


def reference(a_proj, b_proj, ln2_w, ln2_b):
    at = np.ascontiguousarray(f64(a_proj).transpose(2, 0, 1))
    bt = np.ascontiguousarray(f64(b_proj).transpose(2, 1, 0))
    tri = mxq(at, 2, "e4m3") @ mxq(bt, 1, "e4m3")
    return layernorm(tri.transpose(1, 2, 0), f64(ln2_w), f64(ln2_b))

@@ -1,0 +1,151 @@
+from contextlib import ExitStack
+
+import concourse.mybir as mybir
+
+FLOPS = 2 * 64 * 128 * 128 * 512
+
+FP8X4 = mybir.dt.float8_e4m3fn_x4
+BF16 = mybir.dt.bfloat16
+F32 = mybir.dt.float32
+U32 = mybir.dt.uint32
+U8 = mybir.dt.uint8
+ALU = mybir.AluOpType
+ACT = mybir.ActivationFunctionType
+
+P = 128
+C = 128
+EPS = 1e-5
+ENG_B = ("v", "v", "s", "s")
+ENG_A = ("v", "s")
+Q_ORDER = ((2, 3, 0, 1), (0, 1, 2, 3))
+
+
+def shuffle(nc, eng, dst, src):
+    o = dst.rearrange("p (g f) r -> p g r f", f=4)
+    i = src.rearrange("p r (g f) -> p g r f", f=4)
+    if eng == "v":
+        nc.vector.tensor_copy(out=o, in_=i)
+    else:
+        nc.scalar.copy(out=o, in_=i)
+
+
+def tile_trianglemultiplication_pa_kernel(tc, a_proj, b_proj, ln2_w, ln2_b, out):
+    nc = tc.nc
+    with ExitStack() as ctx:
+        keep = ctx.enter_context(tc.tile_pool(name="keep", bufs=1))
+        stage = ctx.enter_context(tc.tile_pool(name="stage", bufs=3))
+        dpool = ctx.enter_context(tc.tile_pool(name="dpool", bufs=1))
+        opool = ctx.enter_context(tc.tile_pool(name="opool", bufs=3))
+        small = ctx.enter_context(tc.tile_pool(name="small", bufs=2))
+        psum = ctx.enter_context(tc.psum_pool(name="psum", bufs=8))
+
+        codes_b = keep.tile([P, C * 128], U32, align_bytes=64)
+        scales_b = keep.tile([P, C * 128], U8, align_bytes=64)
+        codes_a = [keep.tile([P, C * 32], U32, name="codes_a%d" % h, align_bytes=64) for h in range(2)]
+        scales_a = [keep.tile([P, C * 32], U8, name="scales_a%d" % h, align_bytes=64) for h in range(2)]
+
+        wb_row = keep.tile([P, 256], BF16)
+        nc.vector.memset(wb_row[:], 0.0)
+        nc.scalar.dma_start(out=wb_row[0:1, 0:128], in_=ln2_w.unsqueeze(0))
+        nc.scalar.dma_start(out=wb_row[0:1, 128:256], in_=ln2_b.unsqueeze(0))
+        ones = keep.tile([P, P], BF16)
+        nc.vector.memset(ones[:], 1.0)
+        warm = keep.tile([P, 1], F32)
+        nc.vector.memset(warm[:], 1.0)
+        nc.scalar.activation(out=warm[:], in_=warm[:], func=ACT.Sqrt)
+        ps_wb = psum.tile([P, 512], F32, name="ps")
+        nc.tensor.matmul(out=ps_wb[:, 0:256], lhsT=ones[:], rhs=wb_row[:], start=True, stop=True)
+        wb = keep.tile([P, 256], F32)
+        nc.vector.tensor_copy(out=wb[:], in_=ps_wb[:, 0:256])
+
+        def load(src, n0):
+            raw = stage.tile([P, 8, 512], BF16, name="raw")
+            nc.sync.dma_start(out=raw[:], in_=src[n0 : n0 + 8].rearrange("n (p t) c -> p n (t c)", t=4))
+            return raw[:].rearrange("p n (t c) -> p (n t) c", c=C)
+
+        for h in range(2):
+            d = [dpool.tile([P, 32, 256], BF16, name="d%d" % t, tag="d%d" % t, align_bytes=64) for t in range(4)]
+            for q in range(8):
+                rows = load(b_proj, 64 * h + 8 * q)
+                for t in range(4):
+                    shuffle(nc, ENG_B[t], d[t][:, :, 32 * q : 32 * q + 32], rows[:, :, 32 * t : 32 * t + 32])
+            for t in Q_ORDER[h]:
+                for cl in range(32):
+                    col = (32 * t + cl) * 128 + 64 * h
+                    nc.vector.quantize_mx(
+                        out=codes_b[:, col : col + 64].bitcast(FP8X4),
+                        scales=scales_b[:, col : col + 64],
+                        in_=d[t][:, cl, :],
+                    )
+
+        xs = []
+        for h in range(2):
+            da = [dpool.tile([P, 64, 128], BF16, name="d%d" % u, tag="d%d" % u, align_bytes=64) for u in range(2)]
+            for q in range(4):
+                rows = load(a_proj, 32 * h + 8 * q)
+                for u in range(2):
+                    shuffle(nc, ENG_A[u], da[u][:, :, 32 * q : 32 * q + 32], rows[:, :, 64 * u : 64 * u + 64])
+            for u in range(2):
+                for n in range(2):
+                    col = (64 * u + 32 * n) * 32
+                    nc.vector.quantize_mx(
+                        out=codes_a[h][:, col : col + 1024].bitcast(FP8X4),
+                        scales=scales_a[h][:, col : col + 1024],
+                        in_=da[u][:, 32 * n : 32 * n + 32, :].rearrange("p c r -> p (c r)"),
+                    )
+            x = dpool.tile([P, 32, C], F32, name="x%d" % h, tag="d%d" % (2 + h), align_bytes=64)
+            xs.append(x)
+            for g in range(32):
+                ps = psum.tile([P, 512], F32, name="ps")
+                for s in range(4):
+                    c = 4 * g + s
+                    nc.tensor.matmul_mx(
+                        out=ps[:, 96 * s : 96 * s + 128],
+                        lhsT=codes_b[:, c * 128 : (c + 1) * 128].bitcast(FP8X4),
+                        lhsT_scale=scales_b[:, c * 128 : (c + 1) * 128],
+                        rhs=codes_a[h][:, g * 128 : (g + 1) * 128].bitcast(FP8X4),
+                        rhs_scale=scales_a[h][:, g * 128 : (g + 1) * 128],
+                        start=True,
+                        stop=True,
+                    )
+                good = ps[:].rearrange("p (s y) -> p s y", y=128)[:, :, 0:32]
+                nc.scalar.copy(out=x[:, :, 4 * g : 4 * g + 4], in_=good.rearrange("p s i -> p i s"))
+
+        for h in range(2):
+            x = xs[h]
+            st = small.tile([P, 32, 6], F32, name="st")
+            for i in range(32):
+                nc.vector.bn_stats(out=st[:, i, :], in_=x[:, i, :])
+            msum = small.tile([P, 32], F32, name="msum")
+            mean = small.tile([P, 32], F32, name="mean")
+            diff = small.tile([P, 32], F32, name="diff")
+            dsq = small.tile([P, 32], F32, name="dsq")
+            m2 = small.tile([P, 32], F32, name="m2")
+            var = small.tile([P, 32], F32, name="var")
+            sd = small.tile([P, 32], F32, name="sd")
+            rstd = small.tile([P, 32], F32, name="rstd")
+            nc.vector.tensor_tensor(out=msum[:], in0=st[:, :, 1], in1=st[:, :, 4], op=ALU.add)
+            nc.vector.tensor_scalar(out=mean[:], in0=msum[:], scalar1=0.5, scalar2=None, op0=ALU.mult)
+            nc.vector.tensor_tensor(out=diff[:], in0=st[:, :, 1], in1=st[:, :, 4], op=ALU.subtract)
+            nc.vector.tensor_tensor(out=dsq[:], in0=diff[:], in1=diff[:], op=ALU.mult)
+            nc.vector.tensor_tensor(out=m2[:], in0=st[:, :, 2], in1=st[:, :, 5], op=ALU.add)
+            nc.vector.tensor_scalar(out=m2[:], in0=m2[:], scalar1=1.0 / C, scalar2=EPS, op0=ALU.mult, op1=ALU.add)
+            nc.vector.scalar_tensor_tensor(out=var[:], in0=dsq[:], scalar=0.25, in1=m2[:], op0=ALU.mult, op1=ALU.add)
+            nc.scalar.activation(out=sd[:], in_=var[:], func=ACT.Sqrt)
+            nc.vector.reciprocal(out=rstd[:], in_=sd[:])
+            for g in range(4):
+                o = opool.tile([P, 8, C], F32, name="o")
+                for ii in range(8):
+                    i = 8 * g + ii
+                    nc.vector.tensor_scalar(
+                        out=o[:, ii, :],
+                        in0=x[:, i, :],
+                        scalar1=mean[:, i : i + 1],
+                        scalar2=rstd[:, i : i + 1],
+                        op0=ALU.subtract,
+                        op1=ALU.mult,
+                    )
+                nc.vector.tensor_tensor(out=o[:], in0=o[:], in1=wb[:, 0:128].unsqueeze(1).to_broadcast([P, 8, C]), op=ALU.mult)
+                nc.gpsimd.tensor_tensor(out=o[:], in0=o[:], in1=wb[:, 128:256].unsqueeze(1).to_broadcast([P, 8, C]), op=ALU.add)
+                i0 = 32 * h + 8 * g
+                nc.sync.dma_start(out=out[i0 : i0 + 8].rearrange("i j c -> j i c"), in_=o[:])

@@ -33,16 +33,13 @@ def tile_trianglemultiplication_pa_kernel(tc, a_proj, b_proj, ln2_w, ln2_b, out)
     nc = tc.nc
     with ExitStack() as ctx:
         keep = ctx.enter_context(tc.tile_pool(name="keep", bufs=1))
-        stage = ctx.enter_context(tc.tile_pool(name="stage", bufs=3))
+        stage = ctx.enter_context(tc.tile_pool(name="stage", bufs=6))
         dpool = ctx.enter_context(tc.tile_pool(name="dpool", bufs=1))
-        opool = ctx.enter_context(tc.tile_pool(name="opool", bufs=3))
         small = ctx.enter_context(tc.tile_pool(name="small", bufs=2))
         psum = ctx.enter_context(tc.psum_pool(name="psum", bufs=8))
 
         codes_b = keep.tile([P, C * 128], U32, align_bytes=64)
         scales_b = keep.tile([P, C * 128], U8, align_bytes=64)
-        codes_a = [keep.tile([P, C * 32], U32, name="codes_a%d" % h, align_bytes=64) for h in range(2)]
-        scales_a = [keep.tile([P, C * 32], U8, name="scales_a%d" % h, align_bytes=64) for h in range(2)]
 
         wb_row = keep.tile([P, 256], BF16)
         nc.vector.memset(wb_row[:], 0.0)
@@ -80,20 +77,21 @@ def tile_trianglemultiplication_pa_kernel(tc, a_proj, b_proj, ln2_w, ln2_b, out)
 
         xs = []
         for h in range(2):
-            da = [dpool.tile([P, 64, 128], BF16, name="d%d" % u, tag="d%d" % u, align_bytes=64) for u in range(2)]
+            da = [dpool.tile([P, 64, 128], BF16, name="d%d" % (2 * h + u), tag="d%d" % (2 * h + u), align_bytes=64) for u in range(2)]
+            codes_a = [keep.tile([P, 1024], U32, name="codes_a%d" % n, tag="codes_a%d" % n, align_bytes=64) for n in range(4)]
+            scales_a = [keep.tile([P, 1024], U8, name="scales_a%d" % n, tag="scales_a%d" % n, align_bytes=64) for n in range(4)]
             for q in range(4):
                 rows = load(a_proj, 32 * h + 8 * q)
                 for u in range(2):
                     shuffle(nc, ENG_A[u], da[u][:, :, 32 * q : 32 * q + 32], rows[:, :, 64 * u : 64 * u + 64])
             for u in range(2):
                 for n in range(2):
-                    col = (64 * u + 32 * n) * 32
                     nc.vector.quantize_mx(
-                        out=codes_a[h][:, col : col + 1024].bitcast(FP8X4),
-                        scales=scales_a[h][:, col : col + 1024],
+                        out=codes_a[2 * u + n][:].bitcast(FP8X4),
+                        scales=scales_a[2 * u + n][:],
                         in_=da[u][:, 32 * n : 32 * n + 32, :].rearrange("p c r -> p (c r)"),
                     )
-            x = dpool.tile([P, 32, C], F32, name="x%d" % h, tag="d%d" % (2 + h), align_bytes=64)
+            x = dpool.tile([P, 32, C], F32, name="x%d" % h, tag="d%d" % h, align_bytes=64)
             xs.append(x)
             for g in range(32):
                 ps = psum.tile([P, 512], F32, name="ps")
@@ -103,8 +101,8 @@ def tile_trianglemultiplication_pa_kernel(tc, a_proj, b_proj, ln2_w, ln2_b, out)
                         out=ps[:, 96 * s : 96 * s + 128],
                         lhsT=codes_b[:, c * 128 : (c + 1) * 128].bitcast(FP8X4),
                         lhsT_scale=scales_b[:, c * 128 : (c + 1) * 128],
-                        rhs=codes_a[h][:, g * 128 : (g + 1) * 128].bitcast(FP8X4),
-                        rhs_scale=scales_a[h][:, g * 128 : (g + 1) * 128],
+                        rhs=codes_a[g // 8][:, (g % 8) * 128 : (g % 8 + 1) * 128].bitcast(FP8X4),
+                        rhs_scale=scales_a[g // 8][:, (g % 8) * 128 : (g % 8 + 1) * 128],
                         start=True,
                         stop=True,
                     )
@@ -134,18 +132,18 @@ def tile_trianglemultiplication_pa_kernel(tc, a_proj, b_proj, ln2_w, ln2_b, out)
             nc.scalar.activation(out=sd[:], in_=var[:], func=ACT.Sqrt)
             nc.vector.reciprocal(out=rstd[:], in_=sd[:])
             for g in range(4):
-                o = opool.tile([P, 8, C], F32, name="o")
+                o = x[:, 8 * g : 8 * g + 8, :]
                 for ii in range(8):
                     i = 8 * g + ii
                     nc.vector.tensor_scalar(
-                        out=o[:, ii, :],
+                        out=x[:, i, :],
                         in0=x[:, i, :],
                         scalar1=mean[:, i : i + 1],
                         scalar2=rstd[:, i : i + 1],
                         op0=ALU.subtract,
                         op1=ALU.mult,
                     )
-                nc.vector.tensor_tensor(out=o[:], in0=o[:], in1=wb[:, 0:128].unsqueeze(1).to_broadcast([P, 8, C]), op=ALU.mult)
-                nc.gpsimd.tensor_tensor(out=o[:], in0=o[:], in1=wb[:, 128:256].unsqueeze(1).to_broadcast([P, 8, C]), op=ALU.add)
+                nc.vector.tensor_tensor(out=o, in0=o, in1=wb[:, 0:128].unsqueeze(1).to_broadcast([P, 8, C]), op=ALU.mult)
+                nc.gpsimd.tensor_tensor(out=o, in0=o, in1=wb[:, 128:256].unsqueeze(1).to_broadcast([P, 8, C]), op=ALU.add)
                 i0 = 32 * h + 8 * g
-                nc.sync.dma_start(out=out[i0 : i0 + 8].rearrange("i j c -> j i c"), in_=o[:])
+                nc.sync.dma_start(out=out[i0 : i0 + 8].rearrange("i j c -> j i c"), in_=o)

@@ -131,19 +131,20 @@ def tile_trianglemultiplication_pa_kernel(tc, a_proj, b_proj, ln2_w, ln2_b, out)
             nc.vector.scalar_tensor_tensor(out=var[:], in0=dsq[:], scalar=0.25, in1=m2[:], op0=ALU.mult, op1=ALU.add)
             nc.scalar.activation(out=sd[:], in_=var[:], func=ACT.Sqrt)
             nc.vector.reciprocal(out=rstd[:], in_=sd[:])
+            nmr = small.tile([P, 32], F32, name="nmr")
+            nc.vector.scalar_tensor_tensor(out=nmr[:], in0=mean[:], scalar=-1.0, in1=rstd[:], op0=ALU.mult, op1=ALU.mult)
             for g in range(4):
                 o = x[:, 8 * g : 8 * g + 8, :]
                 for ii in range(8):
                     i = 8 * g + ii
-                    nc.vector.tensor_scalar(
+                    nc.scalar.activation(
                         out=x[:, i, :],
-                        in0=x[:, i, :],
-                        scalar1=mean[:, i : i + 1],
-                        scalar2=rstd[:, i : i + 1],
-                        op0=ALU.subtract,
-                        op1=ALU.mult,
+                        in_=x[:, i, :],
+                        func=ACT.Identity,
+                        scale=rstd[:, i : i + 1],
+                        bias=nmr[:, i : i + 1],
                     )
                 nc.vector.tensor_tensor(out=o, in0=o, in1=wb[:, 0:128].unsqueeze(1).to_broadcast([P, 8, C]), op=ALU.mult)
-                nc.gpsimd.tensor_tensor(out=o, in0=o, in1=wb[:, 128:256].unsqueeze(1).to_broadcast([P, 8, C]), op=ALU.add)
+                nc.vector.tensor_tensor(out=o, in0=o, in1=wb[:, 128:256].unsqueeze(1).to_broadcast([P, 8, C]), op=ALU.add)
                 i0 = 32 * h + 8 * g
                 nc.sync.dma_start(out=out[i0 : i0 + 8].rearrange("i j c -> j i c"), in_=o)

@@ -1,6 +1,7 @@
 from contextlib import ExitStack
 
 import concourse.mybir as mybir
+from concourse.masks import make_identity
 
 FLOPS = 2 * 64 * 128 * 128 * 512
 
@@ -36,24 +37,27 @@ def tile_trianglemultiplication_pa_kernel(tc, a_proj, b_proj, ln2_w, ln2_b, out)
         stage = ctx.enter_context(tc.tile_pool(name="stage", bufs=6))
         dpool = ctx.enter_context(tc.tile_pool(name="dpool", bufs=1))
         small = ctx.enter_context(tc.tile_pool(name="small", bufs=2))
+        ypool = ctx.enter_context(tc.tile_pool(name="ypool", bufs=3))
         psum = ctx.enter_context(tc.psum_pool(name="psum", bufs=8))
 
         codes_b = keep.tile([P, C * 128], U32, align_bytes=64)
         scales_b = keep.tile([P, C * 128], U8, align_bytes=64)
 
-        wb_row = keep.tile([P, 256], BF16)
-        nc.vector.memset(wb_row[:], 0.0)
-        nc.scalar.dma_start(out=wb_row[0:1, 0:128], in_=ln2_w.unsqueeze(0))
-        nc.scalar.dma_start(out=wb_row[0:1, 128:256], in_=ln2_b.unsqueeze(0))
-        ones = keep.tile([P, P], BF16)
-        nc.vector.memset(ones[:], 1.0)
+        ident = keep.tile([P, P], F32)
+        make_identity(nc, ident[:])
+        wb_rows = keep.tile([P, P], BF16)
+        nc.vector.memset(wb_rows[:], 0.0)
+        nc.scalar.dma_start(out=wb_rows[0:1, :], in_=ln2_w.unsqueeze(0))
+        nc.scalar.dma_start(out=wb_rows[1:2, :], in_=ln2_b.unsqueeze(0))
+        wb_f32 = keep.tile([P, P], F32)
+        nc.vector.tensor_copy(out=wb_f32[:], in_=wb_rows[:])
         warm = keep.tile([P, 1], F32)
         nc.vector.memset(warm[:], 1.0)
         nc.scalar.activation(out=warm[:], in_=warm[:], func=ACT.Sqrt)
         ps_wb = psum.tile([P, 512], F32, name="ps")
-        nc.tensor.matmul(out=ps_wb[:, 0:256], lhsT=ones[:], rhs=wb_row[:], start=True, stop=True)
-        wb = keep.tile([P, 256], F32)
-        nc.vector.tensor_copy(out=wb[:], in_=ps_wb[:, 0:256])
+        nc.tensor.transpose(out=ps_wb[:, 0:P], in_=wb_f32[:], identity=ident[:])
+        wb_col = keep.tile([P, 2], F32)
+        nc.vector.tensor_copy(out=wb_col[:], in_=ps_wb[:, 0:2])
 
         def load(src, n0):
             raw = stage.tile([P, 8, 512], BF16, name="raw")
@@ -131,20 +135,30 @@ def tile_trianglemultiplication_pa_kernel(tc, a_proj, b_proj, ln2_w, ln2_b, out)
             nc.vector.scalar_tensor_tensor(out=var[:], in0=dsq[:], scalar=0.25, in1=m2[:], op0=ALU.mult, op1=ALU.add)
             nc.scalar.activation(out=sd[:], in_=var[:], func=ACT.Sqrt)
             nc.vector.reciprocal(out=rstd[:], in_=sd[:])
-            nmr = small.tile([P, 32], F32, name="nmr")
-            nc.vector.scalar_tensor_tensor(out=nmr[:], in0=mean[:], scalar=-1.0, in1=rstd[:], op0=ALU.mult, op1=ALU.mult)
-            for g in range(4):
-                o = x[:, 8 * g : 8 * g + 8, :]
-                for ii in range(8):
-                    i = 8 * g + ii
-                    nc.scalar.activation(
+            for g in range(8):
+                i0 = 4 * g
+                for i in range(i0, i0 + 4):
+                    nc.vector.tensor_scalar(
                         out=x[:, i, :],
-                        in_=x[:, i, :],
-                        func=ACT.Identity,
-                        scale=rstd[:, i : i + 1],
-                        bias=nmr[:, i : i + 1],
+                        in0=x[:, i, :],
+                        scalar1=mean[:, i : i + 1],
+                        scalar2=rstd[:, i : i + 1],
+                        op0=ALU.subtract,
+                        op1=ALU.mult,
                     )
-                nc.vector.tensor_tensor(out=o, in0=o, in1=wb[:, 0:128].unsqueeze(1).to_broadcast([P, 8, C]), op=ALU.mult)
-                nc.vector.tensor_tensor(out=o, in0=o, in1=wb[:, 128:256].unsqueeze(1).to_broadcast([P, 8, C]), op=ALU.add)
-                i0 = 32 * h + 8 * g
-                nc.sync.dma_start(out=out[i0 : i0 + 8].rearrange("i j c -> j i c"), in_=o)
+                t1 = psum.tile([P, 512], F32, name="ps")
+                for k in range(4):
+                    nc.tensor.transpose(out=t1[:, P * k : P * (k + 1)], in_=x[:, i0 + k, :], identity=ident[:])
+                y = ypool.tile([P, 512], F32, name="y")
+                nc.scalar.activation(out=y[:], in_=t1[:], func=ACT.Identity, scale=wb_col[:, 0:1], bias=wb_col[:, 1:2])
+                t2 = psum.tile([P, 512], F32, name="ps")
+                for k in range(4):
+                    nc.tensor.transpose(out=t2[:, P * k : P * (k + 1)], in_=y[:, P * k : P * (k + 1)], identity=ident[:])
+                done = x[:, i0 : i0 + 4, :].rearrange("p i c -> p (i c)")
+                if h == 0:
+                    nc.scalar.copy(out=done, in_=t2[:])
+                else:
+                    nc.vector.tensor_copy(out=done, in_=t2[:])
+                if g % 2 == 1:
+                    n0 = 32 * h + i0 - 4
+                    nc.sync.dma_start(out=out[n0 : n0 + 8].rearrange("i j c -> j i c"), in_=x[:, i0 - 4 : i0 + 4, :])

@@ -16,23 +16,12 @@ ACT = mybir.ActivationFunctionType
 P = 128
 C = 128
 EPS = 1e-5
-ENG_B = ("v", "v", "s", "s")
-ENG_A = ("v", "s")
-Q_ORDER = ((2, 3, 0, 1), (0, 1, 2, 3))
-
-
-def shuffle(nc, eng, dst, src):
-    o = dst.rearrange("p (g f) r -> p g r f", f=4)
-    i = src.rearrange("p r (g f) -> p g r f", f=4)
-    if eng == "v":
-        nc.vector.tensor_copy(out=o, in_=i)
-    else:
-        nc.scalar.copy(out=o, in_=i)
 
 
 def tile_trianglemultiplication_pa_kernel(tc, a_proj, b_proj, ln2_w, ln2_b, out):
     nc = tc.nc
     with ExitStack() as ctx:
+        ctx.enter_context(tc.manual_schedule())
         keep = ctx.enter_context(tc.tile_pool(name="keep", bufs=1))
         stage = ctx.enter_context(tc.tile_pool(name="stage", bufs=6))
         dpool = ctx.enter_context(tc.tile_pool(name="dpool", bufs=1))
@@ -43,78 +32,120 @@ def tile_trianglemultiplication_pa_kernel(tc, a_proj, b_proj, ln2_w, ln2_b, out)
         codes_b = keep.tile([P, C * 128], U32, align_bytes=64)
         scales_b = keep.tile([P, C * 128], U8, align_bytes=64)
 
-        ident = keep.tile([P, P], F32)
-        make_identity(nc, ident[:])
-        wb_rows = keep.tile([P, P], BF16)
-        nc.vector.memset(wb_rows[:], 0.0)
-        nc.scalar.dma_start(out=wb_rows[0:1, :], in_=ln2_w.unsqueeze(0))
-        nc.scalar.dma_start(out=wb_rows[1:2, :], in_=ln2_b.unsqueeze(0))
-        wb_f32 = keep.tile([P, P], F32)
-        nc.vector.tensor_copy(out=wb_f32[:], in_=wb_rows[:])
-        warm = keep.tile([P, 1], F32)
-        nc.vector.memset(warm[:], 1.0)
-        nc.scalar.activation(out=warm[:], in_=warm[:], func=ACT.Sqrt)
-        ps_wb = psum.tile([P, 512], F32, name="ps")
-        nc.tensor.transpose(out=ps_wb[:, 0:P], in_=wb_f32[:], identity=ident[:])
-        wb_col = keep.tile([P, 2], F32)
-        nc.vector.tensor_copy(out=wb_col[:], in_=ps_wb[:, 0:2])
-
         def load(src, n0):
             raw = stage.tile([P, 8, 512], BF16, name="raw")
             nc.sync.dma_start(out=raw[:], in_=src[n0 : n0 + 8].rearrange("n (p t) c -> p n (t c)", t=4))
             return raw[:].rearrange("p n (t c) -> p (n t) c", c=C)
 
-        for h in range(2):
-            d = [dpool.tile([P, 32, 256], BF16, name="d%d" % t, tag="d%d" % t, align_bytes=64) for t in range(4)]
+        def regroup(copy, dst, src):
+            copy(out=dst.rearrange("p (g f) r -> p g r f", f=4), in_=src.rearrange("p r (g f) -> p g r f", f=4))
+
+        def slot(t, shape, dtype):
+            return dpool.tile(shape, dtype, name="d%d" % t, tag="d%d" % t, align_bytes=64)
+
+        wb_rows = keep.tile([P, P], BF16)
+        nc.vector.memset(wb_rows[:], 0.0)
+        nc.scalar.dma_start(out=wb_rows[0:1, :], in_=ln2_w.unsqueeze(0))
+        nc.scalar.dma_start(out=wb_rows[1:2, :], in_=ln2_b.unsqueeze(0))
+        warm = keep.tile([P, 1], F32)
+        nc.vector.memset(warm[:], 1.0)
+        nc.scalar.activation(out=warm[:], in_=warm[:], func=ACT.Sqrt)
+        ident = keep.tile([P, P], F32)
+        make_identity(nc, ident[:])
+
+        def b_half(h):
+            d = [slot(t, [P, 32, 256], BF16) for t in range(4)]
             for q in range(8):
                 rows = load(b_proj, 64 * h + 8 * q)
                 for t in range(4):
-                    shuffle(nc, ENG_B[t], d[t][:, :, 32 * q : 32 * q + 32], rows[:, :, 32 * t : 32 * t + 32])
-            for t in Q_ORDER[h]:
-                for cl in range(32):
-                    col = (32 * t + cl) * 128 + 64 * h
-                    nc.vector.quantize_mx(
-                        out=codes_b[:, col : col + 64].bitcast(FP8X4),
-                        scales=scales_b[:, col : col + 64],
-                        in_=d[t][:, cl, :],
-                    )
+                    copy = nc.vector.tensor_copy if t < 2 else nc.scalar.copy
+                    regroup(copy, d[t][:, :, 32 * q : 32 * q + 32], rows[:, :, 32 * t : 32 * t + 32])
+            return d
 
-        xs = []
-        for h in range(2):
-            da = [dpool.tile([P, 64, 128], BF16, name="d%d" % (2 * h + u), tag="d%d" % (2 * h + u), align_bytes=64) for u in range(2)]
+        def quantise_b(h, d, t):
+            for cl in range(32):
+                col = (32 * t + cl) * 128 + 64 * h
+                nc.vector.quantize_mx(
+                    out=codes_b[:, col : col + 64].bitcast(FP8X4),
+                    scales=scales_b[:, col : col + 64],
+                    in_=d[t][:, cl, :],
+                )
+
+        d = b_half(0)
+        for t in (0, 2, 3, 1):
+            quantise_b(0, d, t)
+
+        wb_f32 = keep.tile([P, P], F32)
+        nc.vector.tensor_copy(out=wb_f32[:], in_=wb_rows[:])
+        ps_wb = psum.tile([P, 512], F32, name="ps")
+        nc.tensor.transpose(out=ps_wb[:, 0:P], in_=wb_f32[:], identity=ident[:])
+        wb_col = keep.tile([P, 2], F32)
+        nc.vector.tensor_copy(out=wb_col[:], in_=ps_wb[:, 0:2])
+
+        d = b_half(1)
+
+        def quantise_a(da, codes_a, scales_a, n):
+            nc.vector.quantize_mx(
+                out=codes_a[n][:].bitcast(FP8X4),
+                scales=scales_a[n][:],
+                in_=da[n // 2][:, 32 * (n % 2) : 32 * (n % 2) + 32, :].rearrange("p c r -> p (c r)"),
+            )
+
+        def a_codes():
             codes_a = [keep.tile([P, 1024], U32, name="codes_a%d" % n, tag="codes_a%d" % n, align_bytes=64) for n in range(4)]
             scales_a = [keep.tile([P, 1024], U8, name="scales_a%d" % n, tag="scales_a%d" % n, align_bytes=64) for n in range(4)]
-            for q in range(4):
-                rows = load(a_proj, 32 * h + 8 * q)
-                for u in range(2):
-                    shuffle(nc, ENG_A[u], da[u][:, :, 32 * q : 32 * q + 32], rows[:, :, 64 * u : 64 * u + 64])
-            for u in range(2):
-                for n in range(2):
-                    nc.vector.quantize_mx(
-                        out=codes_a[2 * u + n][:].bitcast(FP8X4),
-                        scales=scales_a[2 * u + n][:],
-                        in_=da[u][:, 32 * n : 32 * n + 32, :].rearrange("p c r -> p (c r)"),
-                    )
-            x = dpool.tile([P, 32, C], F32, name="x%d" % h, tag="d%d" % h, align_bytes=64)
-            xs.append(x)
-            for g in range(32):
-                ps = psum.tile([P, 512], F32, name="ps")
-                for s in range(4):
-                    c = 4 * g + s
-                    nc.tensor.matmul_mx(
-                        out=ps[:, 96 * s : 96 * s + 128],
-                        lhsT=codes_b[:, c * 128 : (c + 1) * 128].bitcast(FP8X4),
-                        lhsT_scale=scales_b[:, c * 128 : (c + 1) * 128],
-                        rhs=codes_a[g // 8][:, (g % 8) * 128 : (g % 8 + 1) * 128].bitcast(FP8X4),
-                        rhs_scale=scales_a[g // 8][:, (g % 8) * 128 : (g % 8 + 1) * 128],
-                        start=True,
-                        stop=True,
-                    )
-                good = ps[:].rearrange("p (s y) -> p s y", y=128)[:, :, 0:32]
-                nc.scalar.copy(out=x[:, :, 4 * g : 4 * g + 4], in_=good.rearrange("p s i -> p i s"))
+            return codes_a, scales_a
 
-        for h in range(2):
-            x = xs[h]
+        def bank(x, codes_a, scales_a, g):
+            ps = psum.tile([P, 512], F32, name="ps")
+            for s in range(4):
+                c = 4 * g + s
+                nc.tensor.matmul_mx(
+                    out=ps[:, 96 * s : 96 * s + 128],
+                    lhsT=codes_b[:, c * 128 : (c + 1) * 128].bitcast(FP8X4),
+                    lhsT_scale=scales_b[:, c * 128 : (c + 1) * 128],
+                    rhs=codes_a[g // 8][:, (g % 8) * 128 : (g % 8 + 1) * 128].bitcast(FP8X4),
+                    rhs_scale=scales_a[g // 8][:, (g % 8) * 128 : (g % 8 + 1) * 128],
+                    start=True,
+                    stop=True,
+                )
+            good = ps[:].rearrange("p (s y) -> p s y", y=128)[:, :, 0:32]
+            nc.scalar.copy(out=x[:, :, 4 * g : 4 * g + 4], in_=good.rearrange("p s i -> p i s"))
+
+        rows1 = [load(a_proj, 8 * q) for q in range(4)]
+        quantise_b(1, d, 0)
+        da1 = [slot(0, [P, 64, 128], BF16)]
+        for q in range(4):
+            regroup(nc.scalar.copy, da1[0][:, :, 32 * q : 32 * q + 32], rows1[q][:, :, 0:64])
+        quantise_b(1, d, 1)
+        da1.append(slot(1, [P, 64, 128], BF16))
+        quantise_b(1, d, 2)
+        quantise_b(1, d, 3)
+        for q in range(4):
+            regroup(nc.vector.tensor_copy, da1[1][:, :, 32 * q : 32 * q + 32], rows1[q][:, :, 64:128])
+        rows2 = [load(a_proj, 32 + 8 * q) for q in range(4)]
+        codes_a, scales_a = a_codes()
+        for n in range(4):
+            quantise_a(da1, codes_a, scales_a, n)
+        x0 = slot(0, [P, 32, C], F32)
+        x1 = slot(1, [P, 32, C], F32)
+        da2 = [slot(2, [P, 64, 128], BF16), slot(3, [P, 64, 128], BF16)]
+        regroup(nc.scalar.copy, da2[0][:, :, 0:32], rows2[0][:, :, 0:64])
+        for q in range(1, 4):
+            regroup(nc.scalar.copy, da2[0][:, :, 32 * q : 32 * q + 32], rows2[q][:, :, 0:64])
+            for g in range(8 * (q - 1), 8 * q):
+                bank(x0, codes_a, scales_a, g)
+        for g in range(24, 32):
+            bank(x0, codes_a, scales_a, g)
+        for q in range(4):
+            regroup(nc.vector.tensor_copy, da2[1][:, :, 32 * q : 32 * q + 32], rows2[q][:, :, 64:128])
+        codes_a, scales_a = a_codes()
+        for n in range(4):
+            quantise_a(da2, codes_a, scales_a, n)
+        for g in range(32):
+            bank(x1, codes_a, scales_a, g)
+
+        def stats(x):
             st = small.tile([P, 32, 6], F32, name="st")
             for i in range(32):
                 nc.vector.bn_stats(out=st[:, i, :], in_=x[:, i, :])
@@ -126,18 +157,23 @@ def tile_trianglemultiplication_pa_kernel(tc, a_proj, b_proj, ln2_w, ln2_b, out)
             var = small.tile([P, 32], F32, name="var")
             sd = small.tile([P, 32], F32, name="sd")
             rstd = small.tile([P, 32], F32, name="rstd")
-            nc.vector.tensor_tensor(out=msum[:], in0=st[:, :, 1], in1=st[:, :, 4], op=ALU.add)
-            nc.vector.tensor_scalar(out=mean[:], in0=msum[:], scalar1=0.5, scalar2=None, op0=ALU.mult)
             nc.vector.tensor_tensor(out=diff[:], in0=st[:, :, 1], in1=st[:, :, 4], op=ALU.subtract)
             nc.vector.tensor_tensor(out=dsq[:], in0=diff[:], in1=diff[:], op=ALU.mult)
             nc.vector.tensor_tensor(out=m2[:], in0=st[:, :, 2], in1=st[:, :, 5], op=ALU.add)
             nc.vector.tensor_scalar(out=m2[:], in0=m2[:], scalar1=1.0 / C, scalar2=EPS, op0=ALU.mult, op1=ALU.add)
             nc.vector.scalar_tensor_tensor(out=var[:], in0=dsq[:], scalar=0.25, in1=m2[:], op0=ALU.mult, op1=ALU.add)
             nc.scalar.activation(out=sd[:], in_=var[:], func=ACT.Sqrt)
+            nc.vector.tensor_tensor(out=msum[:], in0=st[:, :, 1], in1=st[:, :, 4], op=ALU.add)
+            nc.vector.tensor_scalar(out=mean[:], in0=msum[:], scalar1=0.5, scalar2=None, op0=ALU.mult)
             nc.vector.reciprocal(out=rstd[:], in_=sd[:])
-            for g in range(8):
-                i0 = 4 * g
-                for i in range(i0, i0 + 4):
+            return mean, rstd
+
+        def finish(h, x, mean, rstd):
+            t1 = {}
+            y = {}
+
+            def normalise_and_turn(g):
+                for i in range(4 * g, 4 * g + 4):
                     nc.vector.tensor_scalar(
                         out=x[:, i, :],
                         in0=x[:, i, :],
@@ -146,19 +182,34 @@ def tile_trianglemultiplication_pa_kernel(tc, a_proj, b_proj, ln2_w, ln2_b, out)
                         op0=ALU.subtract,
                         op1=ALU.mult,
                     )
-                t1 = psum.tile([P, 512], F32, name="ps")
+                t1[g] = psum.tile([P, 512], F32, name="ps")
                 for k in range(4):
-                    nc.tensor.transpose(out=t1[:, P * k : P * (k + 1)], in_=x[:, i0 + k, :], identity=ident[:])
-                y = ypool.tile([P, 512], F32, name="y")
-                nc.scalar.activation(out=y[:], in_=t1[:], func=ACT.Identity, scale=wb_col[:, 0:1], bias=wb_col[:, 1:2])
+                    nc.tensor.transpose(out=t1[g][:, P * k : P * (k + 1)], in_=x[:, 4 * g + k, :], identity=ident[:])
+
+            def gain_and_bias(g):
+                y[g] = ypool.tile([P, 512], F32, name="y")
+                nc.scalar.activation(out=y[g][:], in_=t1[g][:], func=ACT.Identity, scale=wb_col[:, 0:1], bias=wb_col[:, 1:2])
+
+            def turn_back_and_store(g):
                 t2 = psum.tile([P, 512], F32, name="ps")
                 for k in range(4):
-                    nc.tensor.transpose(out=t2[:, P * k : P * (k + 1)], in_=y[:, P * k : P * (k + 1)], identity=ident[:])
-                done = x[:, i0 : i0 + 4, :].rearrange("p i c -> p (i c)")
-                if h == 0:
-                    nc.scalar.copy(out=done, in_=t2[:])
-                else:
-                    nc.vector.tensor_copy(out=done, in_=t2[:])
+                    nc.tensor.transpose(out=t2[:, P * k : P * (k + 1)], in_=y[g][:, P * k : P * (k + 1)], identity=ident[:])
+                nc.scalar.copy(out=x[:, 4 * g : 4 * g + 4, :].rearrange("p i c -> p (i c)"), in_=t2[:])
                 if g % 2 == 1:
-                    n0 = 32 * h + i0 - 4
-                    nc.sync.dma_start(out=out[n0 : n0 + 8].rearrange("i j c -> j i c"), in_=x[:, i0 - 4 : i0 + 4, :])
+                    n0 = 32 * h + 4 * g - 4
+                    nc.sync.dma_start(out=out[n0 : n0 + 8].rearrange("i j c -> j i c"), in_=x[:, 4 * g - 4 : 4 * g + 4, :])
+
+            normalise_and_turn(0)
+            normalise_and_turn(1)
+            gain_and_bias(0)
+            for g in range(8):
+                if g + 2 < 8:
+                    normalise_and_turn(g + 2)
+                if g + 1 < 8:
+                    gain_and_bias(g + 1)
+                turn_back_and_store(g)
+
+        mean, rstd = stats(x0)
+        finish(0, x0, mean, rstd)
+        mean, rstd = stats(x1)
+        finish(1, x1, mean, rstd)

@@ -121,11 +121,15 @@ def tile_trianglemultiplication_pa_kernel(tc, a_proj, b_proj, ln2_w, ln2_b, out)
         da1.append(slot(1, [P, 64, 128], BF16))
         quantise_b(1, d, 2)
         quantise_b(1, d, 3)
-        for q in range(4):
+        codes_a, scales_a = a_codes()
+        for q in range(2):
+            regroup(nc.vector.tensor_copy, da1[1][:, :, 32 * q : 32 * q + 32], rows1[q][:, :, 64:128])
+        for n in range(2):
+            quantise_a(da1, codes_a, scales_a, n)
+        for q in range(2, 4):
             regroup(nc.vector.tensor_copy, da1[1][:, :, 32 * q : 32 * q + 32], rows1[q][:, :, 64:128])
         rows2 = [load(a_proj, 32 + 8 * q) for q in range(4)]
-        codes_a, scales_a = a_codes()
-        for n in range(4):
+        for n in range(2, 4):
             quantise_a(da1, codes_a, scales_a, n)
         x0 = slot(0, [P, 32, C], F32)
         x1 = slot(1, [P, 32, C], F32)
@@ -168,20 +172,11 @@ def tile_trianglemultiplication_pa_kernel(tc, a_proj, b_proj, ln2_w, ln2_b, out)
             nc.vector.reciprocal(out=rstd[:], in_=sd[:])
             return mean, rstd
 
-        def finish(h, x, mean, rstd):
+        def finish(h, x, mean, rstd, copy_out):
             t1 = {}
             y = {}
 
-            def normalise_and_turn(g):
-                for i in range(4 * g, 4 * g + 4):
-                    nc.vector.tensor_scalar(
-                        out=x[:, i, :],
-                        in0=x[:, i, :],
-                        scalar1=mean[:, i : i + 1],
-                        scalar2=rstd[:, i : i + 1],
-                        op0=ALU.subtract,
-                        op1=ALU.mult,
-                    )
+            def turn(g):
                 t1[g] = psum.tile([P, 512], F32, name="ps")
                 for k in range(4):
                     nc.tensor.transpose(out=t1[g][:, P * k : P * (k + 1)], in_=x[:, 4 * g + k, :], identity=ident[:])
@@ -194,22 +189,30 @@ def tile_trianglemultiplication_pa_kernel(tc, a_proj, b_proj, ln2_w, ln2_b, out)
                 t2 = psum.tile([P, 512], F32, name="ps")
                 for k in range(4):
                     nc.tensor.transpose(out=t2[:, P * k : P * (k + 1)], in_=y[g][:, P * k : P * (k + 1)], identity=ident[:])
-                nc.scalar.copy(out=x[:, 4 * g : 4 * g + 4, :].rearrange("p i c -> p (i c)"), in_=t2[:])
-                if g % 2 == 1:
-                    n0 = 32 * h + 4 * g - 4
-                    nc.sync.dma_start(out=out[n0 : n0 + 8].rearrange("i j c -> j i c"), in_=x[:, 4 * g - 4 : 4 * g + 4, :])
+                copy_out(out=x[:, 4 * g : 4 * g + 4, :].rearrange("p i c -> p (i c)"), in_=t2[:])
+                n0 = 32 * h + 4 * g
+                nc.sync.dma_start(out=out[n0 : n0 + 4].rearrange("i j c -> j i c"), in_=x[:, 4 * g : 4 * g + 4, :])
 
-            normalise_and_turn(0)
-            normalise_and_turn(1)
+            for i in range(32):
+                nc.vector.tensor_scalar(
+                    out=x[:, i, :],
+                    in0=x[:, i, :],
+                    scalar1=mean[:, i : i + 1],
+                    scalar2=rstd[:, i : i + 1],
+                    op0=ALU.subtract,
+                    op1=ALU.mult,
+                )
+            turn(0)
+            turn(1)
             gain_and_bias(0)
             for g in range(8):
                 if g + 2 < 8:
-                    normalise_and_turn(g + 2)
+                    turn(g + 2)
                 if g + 1 < 8:
                     gain_and_bias(g + 1)
                 turn_back_and_store(g)
 
         mean, rstd = stats(x0)
-        finish(0, x0, mean, rstd)
+        finish(0, x0, mean, rstd, nc.scalar.copy)
         mean, rstd = stats(x1)
-        finish(1, x1, mean, rstd)
+        finish(1, x1, mean, rstd, nc.vector.tensor_copy)

@@ -112,6 +112,29 @@ def tile_trianglemultiplication_pa_kernel(tc, a_proj, b_proj, ln2_w, ln2_b, out)
             good = ps[:].rearrange("p (s y) -> p s y", y=128)[:, :, 0:32]
             nc.scalar.copy(out=x[:, :, 4 * g : 4 * g + 4], in_=good.rearrange("p s i -> p i s"))
 
+        def stats(x):
+            st = small.tile([P, 32, 6], F32, name="st")
+            for i in range(32):
+                nc.vector.bn_stats(out=st[:, i, :], in_=x[:, i, :])
+            msum = small.tile([P, 32], F32, name="msum")
+            mean = small.tile([P, 32], F32, name="mean")
+            diff = small.tile([P, 32], F32, name="diff")
+            dsq = small.tile([P, 32], F32, name="dsq")
+            m2 = small.tile([P, 32], F32, name="m2")
+            var = small.tile([P, 32], F32, name="var")
+            sd = small.tile([P, 32], F32, name="sd")
+            rstd = small.tile([P, 32], F32, name="rstd")
+            nc.vector.tensor_tensor(out=diff[:], in0=st[:, :, 1], in1=st[:, :, 4], op=ALU.subtract)
+            nc.vector.tensor_tensor(out=dsq[:], in0=diff[:], in1=diff[:], op=ALU.mult)
+            nc.vector.tensor_tensor(out=m2[:], in0=st[:, :, 2], in1=st[:, :, 5], op=ALU.add)
+            nc.vector.tensor_scalar(out=m2[:], in0=m2[:], scalar1=1.0 / C, scalar2=EPS, op0=ALU.mult, op1=ALU.add)
+            nc.vector.scalar_tensor_tensor(out=var[:], in0=dsq[:], scalar=0.25, in1=m2[:], op0=ALU.mult, op1=ALU.add)
+            nc.scalar.activation(out=sd[:], in_=var[:], func=ACT.Sqrt)
+            nc.vector.tensor_tensor(out=msum[:], in0=st[:, :, 1], in1=st[:, :, 4], op=ALU.add)
+            nc.vector.tensor_scalar(out=mean[:], in0=msum[:], scalar1=0.5, scalar2=None, op0=ALU.mult)
+            nc.vector.reciprocal(out=rstd[:], in_=sd[:])
+            return mean, rstd
+
         rows1 = [load(a_proj, 8 * q) for q in range(4)]
         quantise_b(1, d, 0)
         da1 = [slot(0, [P, 64, 128], BF16)]
@@ -146,31 +169,11 @@ def tile_trianglemultiplication_pa_kernel(tc, a_proj, b_proj, ln2_w, ln2_b, out)
         codes_a, scales_a = a_codes()
         for n in range(4):
             quantise_a(da2, codes_a, scales_a, n)
-        for g in range(32):
+        for g in range(24):
             bank(x1, codes_a, scales_a, g)
-
-        def stats(x):
-            st = small.tile([P, 32, 6], F32, name="st")
-            for i in range(32):
-                nc.vector.bn_stats(out=st[:, i, :], in_=x[:, i, :])
-            msum = small.tile([P, 32], F32, name="msum")
-            mean = small.tile([P, 32], F32, name="mean")
-            diff = small.tile([P, 32], F32, name="diff")
-            dsq = small.tile([P, 32], F32, name="dsq")
-            m2 = small.tile([P, 32], F32, name="m2")
-            var = small.tile([P, 32], F32, name="var")
-            sd = small.tile([P, 32], F32, name="sd")
-            rstd = small.tile([P, 32], F32, name="rstd")
-            nc.vector.tensor_tensor(out=diff[:], in0=st[:, :, 1], in1=st[:, :, 4], op=ALU.subtract)
-            nc.vector.tensor_tensor(out=dsq[:], in0=diff[:], in1=diff[:], op=ALU.mult)
-            nc.vector.tensor_tensor(out=m2[:], in0=st[:, :, 2], in1=st[:, :, 5], op=ALU.add)
-            nc.vector.tensor_scalar(out=m2[:], in0=m2[:], scalar1=1.0 / C, scalar2=EPS, op0=ALU.mult, op1=ALU.add)
-            nc.vector.scalar_tensor_tensor(out=var[:], in0=dsq[:], scalar=0.25, in1=m2[:], op0=ALU.mult, op1=ALU.add)
-            nc.scalar.activation(out=sd[:], in_=var[:], func=ACT.Sqrt)
-            nc.vector.tensor_tensor(out=msum[:], in0=st[:, :, 1], in1=st[:, :, 4], op=ALU.add)
-            nc.vector.tensor_scalar(out=mean[:], in0=msum[:], scalar1=0.5, scalar2=None, op0=ALU.mult)
-            nc.vector.reciprocal(out=rstd[:], in_=sd[:])
-            return mean, rstd
+        mean0, rstd0 = stats(x0)
+        for g in range(24, 32):
+            bank(x1, codes_a, scales_a, g)
 
         def finish(h, x, mean, rstd, copy_out):
             t1 = {}
@@ -212,7 +215,6 @@ def tile_trianglemultiplication_pa_kernel(tc, a_proj, b_proj, ln2_w, ln2_b, out)
                     gain_and_bias(g + 1)
                 turn_back_and_store(g)
 
-        mean, rstd = stats(x0)
-        finish(0, x0, mean, rstd, nc.scalar.copy)
+        finish(0, x0, mean0, rstd0, nc.scalar.copy)
         mean, rstd = stats(x1)
         finish(1, x1, mean, rstd, nc.vector.tensor_copy)

@@ -38,7 +38,7 @@ def tile_trianglemultiplication_pa_kernel(tc, a_proj, b_proj, ln2_w, ln2_b, out)
             return raw[:].rearrange("p n (t c) -> p (n t) c", c=C)
 
         def regroup(copy, dst, src):
-            copy(out=dst.rearrange("p (g f) r -> p g r f", f=4), in_=src.rearrange("p r (g f) -> p g r f", f=4))
+            copy(out=dst.rearrange("p (g f) r -> p g r f", f=2), in_=src.rearrange("p r (g f) -> p g r f", f=2))
 
         def slot(t, shape, dtype):
             return dpool.tile(shape, dtype, name="d%d" % t, tag="d%d" % t, align_bytes=64)

@@ -55,11 +55,22 @@ def tile_trianglemultiplication_pa_kernel(tc, a_proj, b_proj, ln2_w, ln2_b, out)
 
         def b_half(h):
             d = [slot(t, [P, 32, 256], BF16) for t in range(4)]
-            for q in range(8):
+            def piece(copy, rows, q, t):
+                regroup(copy, d[t][:, :, 32 * q : 32 * q + 32], rows[:, :, 32 * t : 32 * t + 32])
+
+            first = 0
+            if h == 1:
+                first = 2
+                pair = [load(b_proj, 64 * h + 8 * q) for q in range(2)]
+                for t in (0, 2, 3):
+                    for q in range(2):
+                        piece(nc.scalar.copy, pair[q], q, t)
+                for q in range(2):
+                    piece(nc.vector.tensor_copy, pair[q], q, 1)
+            for q in range(first, 8):
                 rows = load(b_proj, 64 * h + 8 * q)
                 for t in range(4):
-                    copy = nc.vector.tensor_copy if t < 2 else nc.scalar.copy
-                    regroup(copy, d[t][:, :, 32 * q : 32 * q + 32], rows[:, :, 32 * t : 32 * t + 32])
+                    piece(nc.vector.tensor_copy if t < 2 else nc.scalar.copy, rows, q, t)
             return d
 
         def quantise_b(h, d, t):
@@ -175,7 +186,7 @@ def tile_trianglemultiplication_pa_kernel(tc, a_proj, b_proj, ln2_w, ln2_b, out)
         for g in range(24, 32):
             bank(x1, codes_a, scales_a, g)
 
-        def finish(h, x, mean, rstd, copy_out):
+        def finish(h, x, mean, rstd, copy_out, beside):
             t1 = {}
             y = {}
 
@@ -209,12 +220,18 @@ def tile_trianglemultiplication_pa_kernel(tc, a_proj, b_proj, ln2_w, ln2_b, out)
             turn(1)
             gain_and_bias(0)
             for g in range(8):
+                beside(g)
                 if g + 2 < 8:
                     turn(g + 2)
                 if g + 1 < 8:
                     gain_and_bias(g + 1)
                 turn_back_and_store(g)
 
-        finish(0, x0, mean0, rstd0, nc.scalar.copy)
-        mean, rstd = stats(x1)
-        finish(1, x1, mean, rstd, nc.vector.tensor_copy)
+        second = {}
+
+        def stats_of_second(g):
+            if g == 5:
+                second["mean"], second["rstd"] = stats(x1)
+
+        finish(0, x0, mean0, rstd0, nc.scalar.copy, stats_of_second)
+        finish(1, x1, second["mean"], second["rstd"], nc.vector.tensor_copy, lambda g: None)

@@ -109,19 +109,22 @@ def tile_trianglemultiplication_pa_kernel(tc, a_proj, b_proj, ln2_w, ln2_b, out)
 
         def bank(x, codes_a, scales_a, g):
             ps = psum.tile([P, 512], F32, name="ps")
-            for s in range(4):
-                c = 4 * g + s
+            for s in range(8):
+                c = 8 * g + s
+                w0 = ((c % 32) // 2) * 64
+                n = min(128, 1024 - w0)
+                o = 96 * (s // 2) + 32 * (s % 2)
                 nc.tensor.matmul_mx(
-                    out=ps[:, 96 * s : 96 * s + 128],
+                    out=ps[:, o : o + n],
                     lhsT=codes_b[:, c * 128 : (c + 1) * 128].bitcast(FP8X4),
                     lhsT_scale=scales_b[:, c * 128 : (c + 1) * 128],
-                    rhs=codes_a[g // 8][:, (g % 8) * 128 : (g % 8 + 1) * 128].bitcast(FP8X4),
-                    rhs_scale=scales_a[g // 8][:, (g % 8) * 128 : (g % 8 + 1) * 128],
+                    rhs=codes_a[c // 32][:, w0 : w0 + n].bitcast(FP8X4),
+                    rhs_scale=scales_a[c // 32][:, w0 : w0 + n],
                     start=True,
                     stop=True,
                 )
-            good = ps[:].rearrange("p (s y) -> p s y", y=128)[:, :, 0:32]
-            nc.scalar.copy(out=x[:, :, 4 * g : 4 * g + 4], in_=good.rearrange("p s i -> p i s"))
+            good = ps[:, 0:384].rearrange("p (w u i) -> p w u i", u=3, i=32)[:, :, 0:3:2, :]
+            nc.scalar.copy(out=x[:, :, 8 * g : 8 * g + 8].rearrange("p i (w e) -> p i w e", e=2), in_=good.rearrange("p w e i -> p i w e"))
 
         def stats(x):
             st = small.tile([P, 32, 6], F32, name="st")
@@ -171,19 +174,22 @@ def tile_trianglemultiplication_pa_kernel(tc, a_proj, b_proj, ln2_w, ln2_b, out)
         regroup(nc.scalar.copy, da2[0][:, :, 0:32], rows2[0][:, :, 0:64])
         for q in range(1, 4):
             regroup(nc.scalar.copy, da2[0][:, :, 32 * q : 32 * q + 32], rows2[q][:, :, 0:64])
-            for g in range(8 * (q - 1), 8 * q):
+            if q == 3:
+                regroup(nc.scalar.copy, da2[1][:, 0:32, 96:128], rows2[3][:, :, 64:96])
+            for g in range(4 * (q - 1), 4 * q):
                 bank(x0, codes_a, scales_a, g)
-        for g in range(24, 32):
+        for g in range(12, 16):
             bank(x0, codes_a, scales_a, g)
-        for q in range(4):
+        for q in range(3):
             regroup(nc.vector.tensor_copy, da2[1][:, :, 32 * q : 32 * q + 32], rows2[q][:, :, 64:128])
+        regroup(nc.vector.tensor_copy, da2[1][:, 32:64, 96:128], rows2[3][:, :, 96:128])
         codes_a, scales_a = a_codes()
         for n in range(4):
             quantise_a(da2, codes_a, scales_a, n)
-        for g in range(24):
+        for g in range(12):
             bank(x1, codes_a, scales_a, g)
         mean0, rstd0 = stats(x0)
-        for g in range(24, 32):
+        for g in range(12, 16):
             bank(x1, codes_a, scales_a, g)
 
         def finish(h, x, mean, rstd, copy_out, beside):
@@ -230,7 +236,7 @@ def tile_trianglemultiplication_pa_kernel(tc, a_proj, b_proj, ln2_w, ln2_b, out)
         second = {}
 
         def stats_of_second(g):
-            if g == 5:
+            if g == 6:
                 second["mean"], second["rstd"] = stats(x1)
 
         finish(0, x0, mean0, rstd0, nc.scalar.copy, stats_of_second)

@@ -27,6 +27,7 @@ def tile_trianglemultiplication_pa_kernel(tc, a_proj, b_proj, ln2_w, ln2_b, out)
         dpool = ctx.enter_context(tc.tile_pool(name="dpool", bufs=1))
         small = ctx.enter_context(tc.tile_pool(name="small", bufs=2))
         ypool = ctx.enter_context(tc.tile_pool(name="ypool", bufs=3))
+        fpool = ctx.enter_context(tc.tile_pool(name="fpool", bufs=3))
         psum = ctx.enter_context(tc.psum_pool(name="psum", bufs=8))
 
         codes_b = keep.tile([P, C * 128], U32, align_bytes=64)
@@ -203,15 +204,22 @@ def tile_trianglemultiplication_pa_kernel(tc, a_proj, b_proj, ln2_w, ln2_b, out)
 
             def gain_and_bias(g):
                 y[g] = ypool.tile([P, 512], F32, name="y")
-                nc.scalar.activation(out=y[g][:], in_=t1[g][:], func=ACT.Identity, scale=wb_col[:, 0:1], bias=wb_col[:, 1:2])
+                nc.scalar.activation(
+                    out=y[g][:].rearrange("p (l m) -> p l m", l=4),
+                    in_=t1[g][:].rearrange("p (m l) -> p l m", l=4),
+                    func=ACT.Identity,
+                    scale=wb_col[:, 0:1],
+                    bias=wb_col[:, 1:2],
+                )
 
             def turn_back_and_store(g):
                 t2 = psum.tile([P, 512], F32, name="ps")
                 for k in range(4):
                     nc.tensor.transpose(out=t2[:, P * k : P * (k + 1)], in_=y[g][:, P * k : P * (k + 1)], identity=ident[:])
-                copy_out(out=x[:, 4 * g : 4 * g + 4, :].rearrange("p i c -> p (i c)"), in_=t2[:])
+                f = fpool.tile([P, 512], F32, name="f")
+                copy_out(out=f[:], in_=t2[:])
                 n0 = 32 * h + 4 * g
-                nc.sync.dma_start(out=out[n0 : n0 + 4].rearrange("i j c -> j i c"), in_=x[:, 4 * g : 4 * g + 4, :])
+                nc.sync.dma_start(out=out[n0 : n0 + 4].rearrange("i (m l) c -> (i m) (l c)", l=4), in_=f[:])
 
             for i in range(32):
                 nc.vector.tensor_scalar(

@@ -27,7 +27,6 @@ def tile_trianglemultiplication_pa_kernel(tc, a_proj, b_proj, ln2_w, ln2_b, out)
         dpool = ctx.enter_context(tc.tile_pool(name="dpool", bufs=1))
         small = ctx.enter_context(tc.tile_pool(name="small", bufs=2))
         ypool = ctx.enter_context(tc.tile_pool(name="ypool", bufs=3))
-        fpool = ctx.enter_context(tc.tile_pool(name="fpool", bufs=3))
         psum = ctx.enter_context(tc.psum_pool(name="psum", bufs=8))
 
         codes_b = keep.tile([P, C * 128], U32, align_bytes=64)
@@ -216,10 +215,10 @@ def tile_trianglemultiplication_pa_kernel(tc, a_proj, b_proj, ln2_w, ln2_b, out)
                 t2 = psum.tile([P, 512], F32, name="ps")
                 for k in range(4):
                     nc.tensor.transpose(out=t2[:, P * k : P * (k + 1)], in_=y[g][:, P * k : P * (k + 1)], identity=ident[:])
-                f = fpool.tile([P, 512], F32, name="f")
-                copy_out(out=f[:], in_=t2[:])
+                f = x[:, 4 * g : 4 * g + 4, :].rearrange("p i c -> p (i c)")
+                copy_out(out=f, in_=t2[:])
                 n0 = 32 * h + 4 * g
-                nc.sync.dma_start(out=out[n0 : n0 + 4].rearrange("i (m l) c -> (i m) (l c)", l=4), in_=f[:])
+                nc.sync.dma_start(out=out[n0 : n0 + 4].rearrange("i (m l) c -> (i m) (l c)", l=4), in_=f)
 
             for i in range(32):
                 nc.vector.tensor_scalar(

@@ -67,10 +67,18 @@ def tile_trianglemultiplication_pa_kernel(tc, a_proj, b_proj, ln2_w, ln2_b, out)
                         piece(nc.scalar.copy, pair[q], q, t)
                 for q in range(2):
                     piece(nc.vector.tensor_copy, pair[q], q, 1)
-            for q in range(first, 8):
+            for q in range(first, 7):
                 rows = load(b_proj, 64 * h + 8 * q)
                 for t in range(4):
                     piece(nc.vector.tensor_copy if t < 2 else nc.scalar.copy, rows, q, t)
+            raw = stage.tile([P, 8, 512], BF16, name="raw")
+            for e in range(2):
+                n0 = 64 * h + 56 + 4 * e
+                nc.sync.dma_start(out=raw[:, 4 * e : 4 * e + 4, :], in_=b_proj[n0 : n0 + 4].rearrange("n (p t) c -> p n (t c)", t=4))
+                rows = raw[:, 4 * e : 4 * e + 4, :].rearrange("p n (t c) -> p (n t) c", c=C)
+                for t in range(4):
+                    copy = nc.vector.tensor_copy if t < 2 else nc.scalar.copy
+                    regroup(copy, d[t][:, :, 224 + 16 * e : 240 + 16 * e], rows[:, :, 32 * t : 32 * t + 32])
             return d
 
         def quantise_b(h, d, t):

@@ -135,27 +135,15 @@ def tile_trianglemultiplication_pa_kernel(tc, a_proj, b_proj, ln2_w, ln2_b, out)
             nc.scalar.copy(out=x[:, :, 8 * g : 8 * g + 8].rearrange("p i (w e) -> p i w e", e=2), in_=good.rearrange("p w e i -> p i w e"))
 
         def stats(x):
-            st = small.tile([P, 32, 6], F32, name="st")
-            for i in range(32):
-                nc.vector.bn_stats(out=st[:, i, :], in_=x[:, i, :])
-            msum = small.tile([P, 32], F32, name="msum")
-            mean = small.tile([P, 32], F32, name="mean")
-            diff = small.tile([P, 32], F32, name="diff")
-            dsq = small.tile([P, 32], F32, name="dsq")
-            m2 = small.tile([P, 32], F32, name="m2")
-            var = small.tile([P, 32], F32, name="var")
+            st = small.tile([P, 16, 6], F32, name="st")
+            for u in range(16):
+                nc.vector.bn_stats(out=st[:, u, :], in_=x[:, 2 * u : 2 * u + 2, :].rearrange("p i c -> p c i"))
+            fields = st[:].rearrange("p u (e f) -> p (u e) f", f=3)
             sd = small.tile([P, 32], F32, name="sd")
             rstd = small.tile([P, 32], F32, name="rstd")
-            nc.vector.tensor_tensor(out=diff[:], in0=st[:, :, 1], in1=st[:, :, 4], op=ALU.subtract)
-            nc.vector.tensor_tensor(out=dsq[:], in0=diff[:], in1=diff[:], op=ALU.mult)
-            nc.vector.tensor_tensor(out=m2[:], in0=st[:, :, 2], in1=st[:, :, 5], op=ALU.add)
-            nc.vector.tensor_scalar(out=m2[:], in0=m2[:], scalar1=1.0 / C, scalar2=EPS, op0=ALU.mult, op1=ALU.add)
-            nc.vector.scalar_tensor_tensor(out=var[:], in0=dsq[:], scalar=0.25, in1=m2[:], op0=ALU.mult, op1=ALU.add)
-            nc.scalar.activation(out=sd[:], in_=var[:], func=ACT.Sqrt)
-            nc.vector.tensor_tensor(out=msum[:], in0=st[:, :, 1], in1=st[:, :, 4], op=ALU.add)
-            nc.vector.tensor_scalar(out=mean[:], in0=msum[:], scalar1=0.5, scalar2=None, op0=ALU.mult)
+            nc.scalar.activation(out=sd[:], in_=fields[:, :, 2], func=ACT.Sqrt, scale=1.0 / C, bias=EPS)
             nc.vector.reciprocal(out=rstd[:], in_=sd[:])
-            return mean, rstd
+            return fields[:, :, 1], rstd
 
         rows1 = [load(a_proj, 8 * q) for q in range(4)]
         quantise_b(1, d, 0)

@@ -49,7 +49,7 @@ def tile_trianglemultiplication_pa_kernel(tc, a_proj, b_proj, ln2_w, ln2_b, out)
         nc.scalar.dma_start(out=wb_rows[1:2, :], in_=ln2_b.unsqueeze(0))
         warm = keep.tile([P, 1], F32)
         nc.vector.memset(warm[:], 1.0)
-        nc.scalar.activation(out=warm[:], in_=warm[:], func=ACT.Sqrt)
+        nc.scalar.activation(out=warm[:], in_=warm[:], func=ACT.Abs_reciprocal_sqrt)
         ident = keep.tile([P, P], F32)
         make_identity(nc, ident[:])
 
@@ -134,16 +134,16 @@ def tile_trianglemultiplication_pa_kernel(tc, a_proj, b_proj, ln2_w, ln2_b, out)
             good = ps[:, 0:384].rearrange("p (w u i) -> p w u i", u=3, i=32)[:, :, 0:3:2, :]
             nc.scalar.copy(out=x[:, :, 8 * g : 8 * g + 8].rearrange("p i (w e) -> p i w e", e=2), in_=good.rearrange("p w e i -> p i w e"))
 
-        def stats(x):
-            st = small.tile([P, 16, 6], F32, name="st")
-            for u in range(16):
-                nc.vector.bn_stats(out=st[:, u, :], in_=x[:, 2 * u : 2 * u + 2, :].rearrange("p i c -> p c i"))
-            fields = st[:].rearrange("p u (e f) -> p (u e) f", f=3)
-            sd = small.tile([P, 32], F32, name="sd")
-            rstd = small.tile([P, 32], F32, name="rstd")
-            nc.scalar.activation(out=sd[:], in_=fields[:, :, 2], func=ACT.Sqrt, scale=1.0 / C, bias=EPS)
-            nc.vector.reciprocal(out=rstd[:], in_=sd[:])
-            return fields[:, :, 1], rstd
+        def row_stats(x, r0):
+            st = small.tile([P, 8, 6], F32, name="st")
+            for u in range(8):
+                nc.vector.bn_stats(out=st[:, u, :], in_=x[:, r0 + 2 * u : r0 + 2 * u + 2, :].rearrange("p i c -> p c i"))
+            return st[:].rearrange("p u (e f) -> p (u e) f", f=3)
+
+        def inverse_deviation(fields):
+            rstd = small.tile([P, 16], F32, name="rstd")
+            nc.scalar.activation(out=rstd[:], in_=fields[:, :, 2], func=ACT.Abs_reciprocal_sqrt, scale=1.0 / C, bias=EPS)
+            return rstd
 
         rows1 = [load(a_proj, 8 * q) for q in range(4)]
         quantise_b(1, d, 0)
@@ -182,13 +182,19 @@ def tile_trianglemultiplication_pa_kernel(tc, a_proj, b_proj, ln2_w, ln2_b, out)
         codes_a, scales_a = a_codes()
         for n in range(4):
             quantise_a(da2, codes_a, scales_a, n)
-        for g in range(12):
+        first = {}
+        for g in range(9):
             bank(x1, codes_a, scales_a, g)
-        mean0, rstd0 = stats(x0)
-        for g in range(12, 16):
+        first["fa"] = row_stats(x0, 0)
+        first["ra"] = inverse_deviation(first["fa"])
+        for g in range(9, 14):
+            bank(x1, codes_a, scales_a, g)
+        first["fb"] = row_stats(x0, 16)
+        first["rb"] = inverse_deviation(first["fb"])
+        for g in range(14, 16):
             bank(x1, codes_a, scales_a, g)
 
-        def finish(h, x, mean, rstd, copy_out, beside):
+        def finish(h, x, part, copy_out, beside):
             t1 = {}
             y = {}
 
@@ -212,16 +218,17 @@ def tile_trianglemultiplication_pa_kernel(tc, a_proj, b_proj, ln2_w, ln2_b, out)
                 for k in range(4):
                     nc.tensor.transpose(out=t2[:, P * k : P * (k + 1)], in_=y[g][:, P * k : P * (k + 1)], identity=ident[:])
                 f = x[:, 4 * g : 4 * g + 4, :].rearrange("p i c -> p (i c)")
-                copy_out(out=f, in_=t2[:])
+                copy_out(g)(out=f, in_=t2[:])
                 n0 = 32 * h + 4 * g
                 nc.sync.dma_start(out=out[n0 : n0 + 4].rearrange("i (m l) c -> (i m) (l c)", l=4), in_=f)
 
             for i in range(32):
+                fields, rstd = (part["fa"], part["ra"]) if i < 16 else (part["fb"], part["rb"])
                 nc.vector.tensor_scalar(
                     out=x[:, i, :],
                     in0=x[:, i, :],
-                    scalar1=mean[:, i : i + 1],
-                    scalar2=rstd[:, i : i + 1],
+                    scalar1=fields[:, i % 16, 1:2],
+                    scalar2=rstd[:, i % 16 : i % 16 + 1],
                     op0=ALU.subtract,
                     op1=ALU.mult,
                 )
@@ -239,8 +246,12 @@ def tile_trianglemultiplication_pa_kernel(tc, a_proj, b_proj, ln2_w, ln2_b, out)
         second = {}
 
         def stats_of_second(g):
+            if g == 5:
+                second["fa"] = row_stats(x1, 0)
             if g == 6:
-                second["mean"], second["rstd"] = stats(x1)
+                second["ra"] = inverse_deviation(second["fa"])
+                second["fb"] = row_stats(x1, 16)
 
-        finish(0, x0, mean0, rstd0, nc.scalar.copy, stats_of_second)
-        finish(1, x1, second["mean"], second["rstd"], nc.vector.tensor_copy, lambda g: None)
+        finish(0, x0, first, lambda g: nc.scalar.copy, stats_of_second)
+        second["rb"] = inverse_deviation(second["fb"])
+        finish(1, x1, second, lambda g: nc.vector.tensor_copy, lambda g: None)

@@ -16,6 +16,13 @@ ACT = mybir.ActivationFunctionType
 P = 128
 C = 128
 EPS = 1e-5
+SCALAR_ROWS = 12
+RB_AT = 13
+A_AT = 3
+B_AT = 5
+N1_AT = 6
+COPY_V = ()
+COPY_S = ()
 
 
 def tile_trianglemultiplication_pa_kernel(tc, a_proj, b_proj, ln2_w, ln2_b, out):
@@ -134,9 +141,11 @@ def tile_trianglemultiplication_pa_kernel(tc, a_proj, b_proj, ln2_w, ln2_b, out)
             good = ps[:, 0:384].rearrange("p (w u i) -> p w u i", u=3, i=32)[:, :, 0:3:2, :]
             nc.scalar.copy(out=x[:, :, 8 * g : 8 * g + 8].rearrange("p i (w e) -> p i w e", e=2), in_=good.rearrange("p w e i -> p i w e"))
 
-        def row_stats(x, r0):
+        def row_stats(x, r0, between=None):
             st = small.tile([P, 8, 6], F32, name="st")
             for u in range(8):
+                if u == 3 and between is not None:
+                    between()
                 nc.vector.bn_stats(out=st[:, u, :], in_=x[:, r0 + 2 * u : r0 + 2 * u + 2, :].rearrange("p i c -> p c i"))
             return st[:].rearrange("p u (e f) -> p (u e) f", f=3)
 
@@ -187,71 +196,78 @@ def tile_trianglemultiplication_pa_kernel(tc, a_proj, b_proj, ln2_w, ln2_b, out)
             bank(x1, codes_a, scales_a, g)
         first["fa"] = row_stats(x0, 0)
         first["ra"] = inverse_deviation(first["fa"])
-        for g in range(9, 14):
+        bank(x1, codes_a, scales_a, 9)
+
+        def shift_of_first():
+            first["na"] = small.tile([P, 16], F32, name="nshift")
+            nc.vector.scalar_tensor_tensor(out=first["na"][:], in0=first["fa"][:, :, 1], scalar=-1.0, in1=first["ra"][:], op0=ALU.mult, op1=ALU.mult)
+
+        first["fb"] = row_stats(x0, 16, shift_of_first)
+        for g in range(10, 16):
             bank(x1, codes_a, scales_a, g)
-        first["fb"] = row_stats(x0, 16)
-        first["rb"] = inverse_deviation(first["fb"])
-        for g in range(14, 16):
-            bank(x1, codes_a, scales_a, g)
+            for i in range((g - 10) * SCALAR_ROWS // 6, (g - 9) * SCALAR_ROWS // 6):
+                nc.scalar.activation(out=x0[:, i, :], in_=x0[:, i, :], func=ACT.Identity, scale=first["ra"][:, i : i + 1], bias=first["na"][:, i : i + 1])
+            if g == RB_AT:
+                first["rb"] = inverse_deviation(first["fb"])
 
-        def finish(h, x, part, copy_out, beside):
-            t1 = {}
-            y = {}
-
-            def turn(g):
-                t1[g] = psum.tile([P, 512], F32, name="ps")
-                for k in range(4):
-                    nc.tensor.transpose(out=t1[g][:, P * k : P * (k + 1)], in_=x[:, 4 * g + k, :], identity=ident[:])
-
-            def gain_and_bias(g):
-                y[g] = ypool.tile([P, 512], F32, name="y")
-                nc.scalar.activation(
-                    out=y[g][:].rearrange("p (l m) -> p l m", l=4),
-                    in_=t1[g][:].rearrange("p (m l) -> p l m", l=4),
-                    func=ACT.Identity,
-                    scale=wb_col[:, 0:1],
-                    bias=wb_col[:, 1:2],
-                )
-
-            def turn_back_and_store(g):
-                t2 = psum.tile([P, 512], F32, name="ps")
-                for k in range(4):
-                    nc.tensor.transpose(out=t2[:, P * k : P * (k + 1)], in_=y[g][:, P * k : P * (k + 1)], identity=ident[:])
-                f = x[:, 4 * g : 4 * g + 4, :].rearrange("p i c -> p (i c)")
-                copy_out(g)(out=f, in_=t2[:])
-                n0 = 32 * h + 4 * g
-                nc.sync.dma_start(out=out[n0 : n0 + 4].rearrange("i (m l) c -> (i m) (l c)", l=4), in_=f)
-
-            for i in range(32):
-                fields, rstd = (part["fa"], part["ra"]) if i < 16 else (part["fb"], part["rb"])
-                nc.vector.tensor_scalar(
-                    out=x[:, i, :],
-                    in0=x[:, i, :],
-                    scalar1=fields[:, i % 16, 1:2],
-                    scalar2=rstd[:, i % 16 : i % 16 + 1],
-                    op0=ALU.subtract,
-                    op1=ALU.mult,
-                )
-            turn(0)
-            turn(1)
-            gain_and_bias(0)
-            for g in range(8):
-                beside(g)
-                if g + 2 < 8:
-                    turn(g + 2)
-                if g + 1 < 8:
-                    gain_and_bias(g + 1)
-                turn_back_and_store(g)
-
+        xs = (x0, x1)
         second = {}
+        part = (first, second)
+        t1 = {}
+        y = {}
 
-        def stats_of_second(g):
-            if g == 5:
-                second["fa"] = row_stats(x1, 0)
-            if g == 6:
+        def normalise(h, i):
+            fields, rstd = (part[h]["fa"], part[h]["ra"]) if i < 16 else (part[h]["fb"], part[h]["rb"])
+            nc.vector.tensor_scalar(
+                out=xs[h][:, i, :],
+                in0=xs[h][:, i, :],
+                scalar1=fields[:, i % 16, 1:2],
+                scalar2=rstd[:, i % 16 : i % 16 + 1],
+                op0=ALU.subtract,
+                op1=ALU.mult,
+            )
+
+        def turn(u):
+            t1[u] = psum.tile([P, 512], F32, name="ps")
+            for k in range(4):
+                nc.tensor.transpose(out=t1[u][:, P * k : P * (k + 1)], in_=xs[u // 8][:, 4 * (u % 8) + k, :], identity=ident[:])
+
+        def gain_and_bias(u):
+            y[u] = ypool.tile([P, 512], F32, name="y")
+            nc.scalar.activation(
+                out=y[u][:].rearrange("p (l m) -> p l m", l=4),
+                in_=t1[u][:].rearrange("p (m l) -> p l m", l=4),
+                func=ACT.Identity,
+                scale=wb_col[:, 0:1],
+                bias=wb_col[:, 1:2],
+            )
+
+        def turn_back_and_store(u):
+            t2 = psum.tile([P, 512], F32, name="ps")
+            for k in range(4):
+                nc.tensor.transpose(out=t2[:, P * k : P * (k + 1)], in_=y[u][:, P * k : P * (k + 1)], identity=ident[:])
+            f = xs[u // 8][:, 4 * (u % 8) : 4 * (u % 8) + 4, :].rearrange("p i c -> p (i c)")
+            on_vector = (u >= 8 and u not in COPY_S) or u in COPY_V
+            (nc.vector.tensor_copy if on_vector else nc.scalar.copy)(out=f, in_=t2[:])
+            nc.sync.dma_start(out=out[4 * u : 4 * u + 4].rearrange("i (m l) c -> (i m) (l c)", l=4), in_=f)
+
+        for i in range(SCALAR_ROWS, 32):
+            normalise(0, i)
+        second["fa"] = row_stats(x1, 0)
+        second["fb"] = row_stats(x1, 16)
+        turn(0)
+        turn(1)
+        gain_and_bias(0)
+        for u in range(16):
+            if u == A_AT:
                 second["ra"] = inverse_deviation(second["fa"])
-                second["fb"] = row_stats(x1, 16)
-
-        finish(0, x0, first, lambda g: nc.scalar.copy, stats_of_second)
-        second["rb"] = inverse_deviation(second["fb"])
-        finish(1, x1, second, lambda g: nc.vector.tensor_copy, lambda g: None)
+            if u == B_AT:
+                second["rb"] = inverse_deviation(second["fb"])
+            if u == N1_AT:
+                for i in range(32):
+                    normalise(1, i)
+            if u + 2 < 16:
+                turn(u + 2)
+            if u + 1 < 16:
+                gain_and_bias(u + 1)
+            turn_back_and_store(u)

@@ -17,6 +17,7 @@ P = 128
 C = 128
 EPS = 1e-5
 SCALAR_ROWS = 12
+V_MORE = (6,)
 RB_AT = 13
 A_AT = 3
 B_AT = 5
@@ -77,7 +78,7 @@ def tile_trianglemultiplication_pa_kernel(tc, a_proj, b_proj, ln2_w, ln2_b, out)
             for q in range(first, 7):
                 rows = load(b_proj, 64 * h + 8 * q)
                 for t in range(4):
-                    piece(nc.vector.tensor_copy if t < 2 else nc.scalar.copy, rows, q, t)
+                    piece(nc.vector.tensor_copy if t < 2 or (t == 2 and h == 1 and q in V_MORE) else nc.scalar.copy, rows, q, t)
             raw = stage.tile([P, 8, 512], BF16, name="raw")
             for e in range(2):
                 n0 = 64 * h + 56 + 4 * e

@@ -16,14 +16,17 @@ ACT = mybir.ActivationFunctionType
 P = 128
 C = 128
 EPS = 1e-5
-SCALAR_ROWS = 12
+SCALAR_ROWS = 16
 V_MORE = (6,)
-RB_AT = 13
-A_AT = 3
-B_AT = 5
-N1_AT = 6
+RB_AT = 11
+A_AT = 2
+B_AT = 4
+LOOK = 3
 COPY_V = ()
 COPY_S = ()
+GP0 = (6, 7)
+GP1 = ()
+GP0_STORE_AT = 4
 
 
 def tile_trianglemultiplication_pa_kernel(tc, a_proj, b_proj, ln2_w, ln2_b, out):
@@ -54,12 +57,20 @@ def tile_trianglemultiplication_pa_kernel(tc, a_proj, b_proj, ln2_w, ln2_b, out)
         wb_rows = keep.tile([P, P], BF16)
         nc.vector.memset(wb_rows[:], 0.0)
         nc.scalar.dma_start(out=wb_rows[0:1, :], in_=ln2_w.unsqueeze(0))
-        nc.scalar.dma_start(out=wb_rows[1:2, :], in_=ln2_b.unsqueeze(0))
+        nc.scalar.dma_start(out=wb_rows[32:33, :], in_=ln2_b.unsqueeze(0))
+        pick = keep.tile([P, 2, P], BF16)
+        nc.vector.memset(pick[:], 0.0)
+        nc.vector.memset(pick[0:1, 0, :], 1.0)
+        nc.vector.memset(pick[32:33, 1, :], 1.0)
         warm = keep.tile([P, 1], F32)
         nc.vector.memset(warm[:], 1.0)
         nc.scalar.activation(out=warm[:], in_=warm[:], func=ACT.Abs_reciprocal_sqrt)
         ident = keep.tile([P, P], F32)
         make_identity(nc, ident[:])
+
+        wb_f32 = keep.tile([P, P], F32)
+        ps_wb = psum.tile([P, 512], F32, name="ps")
+        wb_all = keep.tile([P, 3 * P], F32)
 
         def b_half(h):
             d = [slot(t, [P, 32, 256], BF16) for t in range(4)]
@@ -79,6 +90,13 @@ def tile_trianglemultiplication_pa_kernel(tc, a_proj, b_proj, ln2_w, ln2_b, out)
                 rows = load(b_proj, 64 * h + 8 * q)
                 for t in range(4):
                     piece(nc.vector.tensor_copy if t < 2 or (t == 2 and h == 1 and q in V_MORE) else nc.scalar.copy, rows, q, t)
+                if h == 0 and q == 3:
+                    nc.vector.tensor_copy(out=wb_f32[:], in_=wb_rows[:])
+                    nc.tensor.transpose(out=ps_wb[:, 0:P], in_=wb_f32[:], identity=ident[:])
+                    for r in range(2):
+                        nc.tensor.matmul(out=ps_wb[:, P * (r + 1) : P * (r + 2)], lhsT=pick[:, r, :], rhs=wb_rows[:], start=True, stop=True)
+                if h == 0 and q == 4:
+                    nc.vector.tensor_copy(out=wb_all[:], in_=ps_wb[:, 0 : 3 * P])
             raw = stage.tile([P, 8, 512], BF16, name="raw")
             for e in range(2):
                 n0 = 64 * h + 56 + 4 * e
@@ -101,13 +119,6 @@ def tile_trianglemultiplication_pa_kernel(tc, a_proj, b_proj, ln2_w, ln2_b, out)
         d = b_half(0)
         for t in (0, 2, 3, 1):
             quantise_b(0, d, t)
-
-        wb_f32 = keep.tile([P, P], F32)
-        nc.vector.tensor_copy(out=wb_f32[:], in_=wb_rows[:])
-        ps_wb = psum.tile([P, 512], F32, name="ps")
-        nc.tensor.transpose(out=ps_wb[:, 0:P], in_=wb_f32[:], identity=ident[:])
-        wb_col = keep.tile([P, 2], F32)
-        nc.vector.tensor_copy(out=wb_col[:], in_=ps_wb[:, 0:2])
 
         d = b_half(1)
 
@@ -239,8 +250,8 @@ def tile_trianglemultiplication_pa_kernel(tc, a_proj, b_proj, ln2_w, ln2_b, out)
                 out=y[u][:].rearrange("p (l m) -> p l m", l=4),
                 in_=t1[u][:].rearrange("p (m l) -> p l m", l=4),
                 func=ACT.Identity,
-                scale=wb_col[:, 0:1],
-                bias=wb_col[:, 1:2],
+                scale=wb_all[:, 0:1],
+                bias=wb_all[:, 32:33],
             )
 
         def turn_back_and_store(u):
@@ -252,23 +263,45 @@ def tile_trianglemultiplication_pa_kernel(tc, a_proj, b_proj, ln2_w, ln2_b, out)
             (nc.vector.tensor_copy if on_vector else nc.scalar.copy)(out=f, in_=t2[:])
             nc.sync.dma_start(out=out[4 * u : 4 * u + 4].rearrange("i (m l) c -> (i m) (l c)", l=4), in_=f)
 
+        def on_gpsimd(us):
+            h, r0, n = us[0] // 8, 4 * (us[0] % 8), 4 * len(us)
+            v = xs[h][:, r0 : r0 + n, :]
+            nc.gpsimd.tensor_tensor(out=v, in0=v, in1=wb_all[:, P : 2 * P].unsqueeze(1).to_broadcast([P, n, C]), op=ALU.mult)
+            nc.gpsimd.tensor_tensor(out=v, in0=v, in1=wb_all[:, 2 * P : 3 * P].unsqueeze(1).to_broadcast([P, n, C]), op=ALU.add)
+
+        def store_rows(us):
+            h, r0, n = us[0] // 8, 4 * (us[0] % 8), 4 * len(us)
+            nc.sync.dma_start(out=out[32 * h + r0 : 32 * h + r0 + n].rearrange("i j c -> j i c"), in_=xs[h][:, r0 : r0 + n, :])
+
         for i in range(SCALAR_ROWS, 32):
             normalise(0, i)
+        if GP0:
+            on_gpsimd(GP0)
         second["fa"] = row_stats(x1, 0)
         second["fb"] = row_stats(x1, 16)
-        turn(0)
-        turn(1)
-        gain_and_bias(0)
-        for u in range(16):
-            if u == A_AT:
+        line = [u for u in range(16) if u not in GP0 and u not in GP1]
+        ready = [0]
+        turn(line[0])
+        turn(line[1])
+        gain_and_bias(line[0])
+        for s in range(len(line)):
+            if s == A_AT:
                 second["ra"] = inverse_deviation(second["fa"])
-            if u == B_AT:
+            if s == B_AT:
                 second["rb"] = inverse_deviation(second["fb"])
-            if u == N1_AT:
-                for i in range(32):
-                    normalise(1, i)
-            if u + 2 < 16:
-                turn(u + 2)
-            if u + 1 < 16:
-                gain_and_bias(u + 1)
-            turn_back_and_store(u)
+            if s + 2 < len(line) and line[s + 2] >= 8:
+                while ready[0] < min(line[s + 2] - 8 + LOOK, 7) + 1:
+                    for i in range(4 * ready[0], 4 * ready[0] + 4):
+                        normalise(1, i)
+                    ready[0] += 1
+                    if GP1 and ready[0] == 8:
+                        on_gpsimd(GP1)
+            if s == GP0_STORE_AT and GP0:
+                store_rows(GP0)
+            if s + 2 < len(line):
+                turn(line[s + 2])
+            if s + 1 < len(line):
+                gain_and_bias(line[s + 1])
+            turn_back_and_store(line[s])
+        if GP1:
+            store_rows(GP1)

@@ -44,7 +44,7 @@ def tile_trianglemultiplication_pa_kernel(tc, a_proj, b_proj, ln2_w, ln2_b, out)
         scales_b = keep.tile([P, C * 128], U8, align_bytes=64)
 
         def load(src, n0):
-            raw = stage.tile([P, 8, 512], BF16, name="raw")
+            raw = stage.tile([P, 8, 512], BF16, name="raw", align_bytes=256)
             nc.sync.dma_start(out=raw[:], in_=src[n0 : n0 + 8].rearrange("n (p t) c -> p n (t c)", t=4))
             return raw[:].rearrange("p n (t c) -> p (n t) c", c=C)
 
@@ -52,7 +52,7 @@ def tile_trianglemultiplication_pa_kernel(tc, a_proj, b_proj, ln2_w, ln2_b, out)
             copy(out=dst.rearrange("p (g f) r -> p g r f", f=2), in_=src.rearrange("p r (g f) -> p g r f", f=2))
 
         def slot(t, shape, dtype):
-            return dpool.tile(shape, dtype, name="d%d" % t, tag="d%d" % t, align_bytes=64)
+            return dpool.tile(shape, dtype, name="d%d" % t, tag="d%d" % t, align_bytes=256)
 
         wb_rows = keep.tile([P, P], BF16)
         nc.vector.memset(wb_rows[:], 0.0)
@@ -97,7 +97,7 @@ def tile_trianglemultiplication_pa_kernel(tc, a_proj, b_proj, ln2_w, ln2_b, out)
                         nc.tensor.matmul(out=ps_wb[:, P * (r + 1) : P * (r + 2)], lhsT=pick[:, r, :], rhs=wb_rows[:], start=True, stop=True)
                 if h == 0 and q == 4:
                     nc.vector.tensor_copy(out=wb_all[:], in_=ps_wb[:, 0 : 3 * P])
-            raw = stage.tile([P, 8, 512], BF16, name="raw")
+            raw = stage.tile([P, 8, 512], BF16, name="raw", align_bytes=256)
             for e in range(2):
                 n0 = 64 * h + 56 + 4 * e
                 nc.sync.dma_start(out=raw[:, 4 * e : 4 * e + 4, :], in_=b_proj[n0 : n0 + 4].rearrange("n (p t) c -> p n (t c)", t=4))

from contextlib import ExitStack

import concourse.mybir as mybir
from concourse.masks import make_identity

FLOPS = 2 * 64 * 128 * 128 * 512

FP8X4 = mybir.dt.float8_e4m3fn_x4
BF16 = mybir.dt.bfloat16
F32 = mybir.dt.float32
U32 = mybir.dt.uint32
U8 = mybir.dt.uint8
ALU = mybir.AluOpType
ACT = mybir.ActivationFunctionType

P = 128
C = 128
EPS = 1e-5
SCALAR_ROWS = 16
V_MORE = (6,)
RB_AT = 11
A_AT = 2
B_AT = 4
LOOK = 3
COPY_V = ()
COPY_S = ()
GP0 = (6, 7)
GP1 = ()
GP0_STORE_AT = 4


def tile_trianglemultiplication_pa_kernel(tc, a_proj, b_proj, ln2_w, ln2_b, out):
    nc = tc.nc
    with ExitStack() as ctx:
        ctx.enter_context(tc.manual_schedule())
        keep = ctx.enter_context(tc.tile_pool(name="keep", bufs=1))
        stage = ctx.enter_context(tc.tile_pool(name="stage", bufs=6))
        dpool = ctx.enter_context(tc.tile_pool(name="dpool", bufs=1))
        small = ctx.enter_context(tc.tile_pool(name="small", bufs=2))
        ypool = ctx.enter_context(tc.tile_pool(name="ypool", bufs=3))
        psum = ctx.enter_context(tc.psum_pool(name="psum", bufs=8))

        codes_b = keep.tile([P, C * 128], U32, align_bytes=64)
        scales_b = keep.tile([P, C * 128], U8, align_bytes=64)

        def load(src, n0):
            raw = stage.tile([P, 8, 512], BF16, name="raw", align_bytes=256)
            nc.sync.dma_start(out=raw[:], in_=src[n0 : n0 + 8].rearrange("n (p t) c -> p n (t c)", t=4))
            return raw[:].rearrange("p n (t c) -> p (n t) c", c=C)

        def regroup(copy, dst, src):
            copy(out=dst.rearrange("p (g f) r -> p g r f", f=2), in_=src.rearrange("p r (g f) -> p g r f", f=2))

        def slot(t, shape, dtype):
            return dpool.tile(shape, dtype, name="d%d" % t, tag="d%d" % t, align_bytes=256)

        wb_rows = keep.tile([P, P], BF16)
        nc.vector.memset(wb_rows[:], 0.0)
        nc.scalar.dma_start(out=wb_rows[0:1, :], in_=ln2_w.unsqueeze(0))
        nc.scalar.dma_start(out=wb_rows[32:33, :], in_=ln2_b.unsqueeze(0))
        pick = keep.tile([P, 2, P], BF16)
        nc.vector.memset(pick[:], 0.0)
        nc.vector.memset(pick[0:1, 0, :], 1.0)
        nc.vector.memset(pick[32:33, 1, :], 1.0)
        warm = keep.tile([P, 1], F32)
        nc.vector.memset(warm[:], 1.0)
        nc.scalar.activation(out=warm[:], in_=warm[:], func=ACT.Abs_reciprocal_sqrt)
        ident = keep.tile([P, P], F32)
        make_identity(nc, ident[:])

        wb_f32 = keep.tile([P, P], F32)
        ps_wb = psum.tile([P, 512], F32, name="ps")
        wb_all = keep.tile([P, 3 * P], F32)

        def b_half(h):
            d = [slot(t, [P, 32, 256], BF16) for t in range(4)]
            def piece(copy, rows, q, t):
                regroup(copy, d[t][:, :, 32 * q : 32 * q + 32], rows[:, :, 32 * t : 32 * t + 32])

            first = 0
            if h == 1:
                first = 2
                pair = [load(b_proj, 64 * h + 8 * q) for q in range(2)]
                for t in (0, 2, 3):
                    for q in range(2):
                        piece(nc.scalar.copy, pair[q], q, t)
                for q in range(2):
                    piece(nc.vector.tensor_copy, pair[q], q, 1)
            for q in range(first, 7):
                rows = load(b_proj, 64 * h + 8 * q)
                for t in range(4):
                    piece(nc.vector.tensor_copy if t < 2 or (t == 2 and h == 1 and q in V_MORE) else nc.scalar.copy, rows, q, t)
                if h == 0 and q == 3:
                    nc.vector.tensor_copy(out=wb_f32[:], in_=wb_rows[:])
                    nc.tensor.transpose(out=ps_wb[:, 0:P], in_=wb_f32[:], identity=ident[:])
                    for r in range(2):
                        nc.tensor.matmul(out=ps_wb[:, P * (r + 1) : P * (r + 2)], lhsT=pick[:, r, :], rhs=wb_rows[:], start=True, stop=True)
                if h == 0 and q == 4:
                    nc.vector.tensor_copy(out=wb_all[:], in_=ps_wb[:, 0 : 3 * P])
            raw = stage.tile([P, 8, 512], BF16, name="raw", align_bytes=256)
            for e in range(2):
                n0 = 64 * h + 56 + 4 * e
                nc.sync.dma_start(out=raw[:, 4 * e : 4 * e + 4, :], in_=b_proj[n0 : n0 + 4].rearrange("n (p t) c -> p n (t c)", t=4))
                rows = raw[:, 4 * e : 4 * e + 4, :].rearrange("p n (t c) -> p (n t) c", c=C)
                for t in range(4):
                    copy = nc.vector.tensor_copy if t < 2 else nc.scalar.copy
                    regroup(copy, d[t][:, :, 224 + 16 * e : 240 + 16 * e], rows[:, :, 32 * t : 32 * t + 32])
            return d

        def quantise_b(h, d, t):
            for cl in range(32):
                col = (32 * t + cl) * 128 + 64 * h
                nc.vector.quantize_mx(
                    out=codes_b[:, col : col + 64].bitcast(FP8X4),
                    scales=scales_b[:, col : col + 64],
                    in_=d[t][:, cl, :],
                )

        d = b_half(0)
        for t in (0, 2, 3, 1):
            quantise_b(0, d, t)

        d = b_half(1)

        def quantise_a(da, codes_a, scales_a, n):
            nc.vector.quantize_mx(
                out=codes_a[n][:].bitcast(FP8X4),
                scales=scales_a[n][:],
                in_=da[n // 2][:, 32 * (n % 2) : 32 * (n % 2) + 32, :].rearrange("p c r -> p (c r)"),
            )

        def a_codes():
            codes_a = [keep.tile([P, 1024], U32, name="codes_a%d" % n, tag="codes_a%d" % n, align_bytes=64) for n in range(4)]
            scales_a = [keep.tile([P, 1024], U8, name="scales_a%d" % n, tag="scales_a%d" % n, align_bytes=64) for n in range(4)]
            return codes_a, scales_a

        def bank(x, codes_a, scales_a, g):
            ps = psum.tile([P, 512], F32, name="ps")
            for s in range(8):
                c = 8 * g + s
                w0 = ((c % 32) // 2) * 64
                n = min(128, 1024 - w0)
                o = 96 * (s // 2) + 32 * (s % 2)
                nc.tensor.matmul_mx(
                    out=ps[:, o : o + n],
                    lhsT=codes_b[:, c * 128 : (c + 1) * 128].bitcast(FP8X4),
                    lhsT_scale=scales_b[:, c * 128 : (c + 1) * 128],
                    rhs=codes_a[c // 32][:, w0 : w0 + n].bitcast(FP8X4),
                    rhs_scale=scales_a[c // 32][:, w0 : w0 + n],
                    start=True,
                    stop=True,
                )
            good = ps[:, 0:384].rearrange("p (w u i) -> p w u i", u=3, i=32)[:, :, 0:3:2, :]
            nc.scalar.copy(out=x[:, :, 8 * g : 8 * g + 8].rearrange("p i (w e) -> p i w e", e=2), in_=good.rearrange("p w e i -> p i w e"))

        def row_stats(x, r0, between=None):
            st = small.tile([P, 8, 6], F32, name="st")
            for u in range(8):
                if u == 3 and between is not None:
                    between()
                nc.vector.bn_stats(out=st[:, u, :], in_=x[:, r0 + 2 * u : r0 + 2 * u + 2, :].rearrange("p i c -> p c i"))
            return st[:].rearrange("p u (e f) -> p (u e) f", f=3)

        def inverse_deviation(fields):
            rstd = small.tile([P, 16], F32, name="rstd")
            nc.scalar.activation(out=rstd[:], in_=fields[:, :, 2], func=ACT.Abs_reciprocal_sqrt, scale=1.0 / C, bias=EPS)
            return rstd

        rows1 = [load(a_proj, 8 * q) for q in range(4)]
        quantise_b(1, d, 0)
        da1 = [slot(0, [P, 64, 128], BF16)]
        for q in range(4):
            regroup(nc.scalar.copy, da1[0][:, :, 32 * q : 32 * q + 32], rows1[q][:, :, 0:64])
        quantise_b(1, d, 1)
        da1.append(slot(1, [P, 64, 128], BF16))
        quantise_b(1, d, 2)
        quantise_b(1, d, 3)
        codes_a, scales_a = a_codes()
        for q in range(2):
            regroup(nc.vector.tensor_copy, da1[1][:, :, 32 * q : 32 * q + 32], rows1[q][:, :, 64:128])
        for n in range(2):
            quantise_a(da1, codes_a, scales_a, n)
        for q in range(2, 4):
            regroup(nc.vector.tensor_copy, da1[1][:, :, 32 * q : 32 * q + 32], rows1[q][:, :, 64:128])
        rows2 = [load(a_proj, 32 + 8 * q) for q in range(4)]
        for n in range(2, 4):
            quantise_a(da1, codes_a, scales_a, n)
        x0 = slot(0, [P, 32, C], F32)
        x1 = slot(1, [P, 32, C], F32)
        da2 = [slot(2, [P, 64, 128], BF16), slot(3, [P, 64, 128], BF16)]
        regroup(nc.scalar.copy, da2[0][:, :, 0:32], rows2[0][:, :, 0:64])
        for q in range(1, 4):
            regroup(nc.scalar.copy, da2[0][:, :, 32 * q : 32 * q + 32], rows2[q][:, :, 0:64])
            if q == 3:
                regroup(nc.scalar.copy, da2[1][:, 0:32, 96:128], rows2[3][:, :, 64:96])
            for g in range(4 * (q - 1), 4 * q):
                bank(x0, codes_a, scales_a, g)
        for g in range(12, 16):
            bank(x0, codes_a, scales_a, g)
        for q in range(3):
            regroup(nc.vector.tensor_copy, da2[1][:, :, 32 * q : 32 * q + 32], rows2[q][:, :, 64:128])
        regroup(nc.vector.tensor_copy, da2[1][:, 32:64, 96:128], rows2[3][:, :, 96:128])
        codes_a, scales_a = a_codes()
        for n in range(4):
            quantise_a(da2, codes_a, scales_a, n)
        first = {}
        for g in range(9):
            bank(x1, codes_a, scales_a, g)
        first["fa"] = row_stats(x0, 0)
        first["ra"] = inverse_deviation(first["fa"])
        bank(x1, codes_a, scales_a, 9)

        def shift_of_first():
            first["na"] = small.tile([P, 16], F32, name="nshift")
            nc.vector.scalar_tensor_tensor(out=first["na"][:], in0=first["fa"][:, :, 1], scalar=-1.0, in1=first["ra"][:], op0=ALU.mult, op1=ALU.mult)

        first["fb"] = row_stats(x0, 16, shift_of_first)
        for g in range(10, 16):
            bank(x1, codes_a, scales_a, g)
            for i in range((g - 10) * SCALAR_ROWS // 6, (g - 9) * SCALAR_ROWS // 6):
                nc.scalar.activation(out=x0[:, i, :], in_=x0[:, i, :], func=ACT.Identity, scale=first["ra"][:, i : i + 1], bias=first["na"][:, i : i + 1])
            if g == RB_AT:
                first["rb"] = inverse_deviation(first["fb"])

        xs = (x0, x1)
        second = {}
        part = (first, second)
        t1 = {}
        y = {}

        def normalise(h, i):
            fields, rstd = (part[h]["fa"], part[h]["ra"]) if i < 16 else (part[h]["fb"], part[h]["rb"])
            nc.vector.tensor_scalar(
                out=xs[h][:, i, :],
                in0=xs[h][:, i, :],
                scalar1=fields[:, i % 16, 1:2],
                scalar2=rstd[:, i % 16 : i % 16 + 1],
                op0=ALU.subtract,
                op1=ALU.mult,
            )

        def turn(u):
            t1[u] = psum.tile([P, 512], F32, name="ps")
            for k in range(4):
                nc.tensor.transpose(out=t1[u][:, P * k : P * (k + 1)], in_=xs[u // 8][:, 4 * (u % 8) + k, :], identity=ident[:])

        def gain_and_bias(u):
            y[u] = ypool.tile([P, 512], F32, name="y")
            nc.scalar.activation(
                out=y[u][:].rearrange("p (l m) -> p l m", l=4),
                in_=t1[u][:].rearrange("p (m l) -> p l m", l=4),
                func=ACT.Identity,
                scale=wb_all[:, 0:1],
                bias=wb_all[:, 32:33],
            )

        def turn_back_and_store(u):
            t2 = psum.tile([P, 512], F32, name="ps")
            for k in range(4):
                nc.tensor.transpose(out=t2[:, P * k : P * (k + 1)], in_=y[u][:, P * k : P * (k + 1)], identity=ident[:])
            f = xs[u // 8][:, 4 * (u % 8) : 4 * (u % 8) + 4, :].rearrange("p i c -> p (i c)")
            on_vector = (u >= 8 and u not in COPY_S) or u in COPY_V
            (nc.vector.tensor_copy if on_vector else nc.scalar.copy)(out=f, in_=t2[:])
            nc.sync.dma_start(out=out[4 * u : 4 * u + 4].rearrange("i (m l) c -> (i m) (l c)", l=4), in_=f)

        def on_gpsimd(us):
            h, r0, n = us[0] // 8, 4 * (us[0] % 8), 4 * len(us)
            v = xs[h][:, r0 : r0 + n, :]
            nc.gpsimd.tensor_tensor(out=v, in0=v, in1=wb_all[:, P : 2 * P].unsqueeze(1).to_broadcast([P, n, C]), op=ALU.mult)
            nc.gpsimd.tensor_tensor(out=v, in0=v, in1=wb_all[:, 2 * P : 3 * P].unsqueeze(1).to_broadcast([P, n, C]), op=ALU.add)

        def store_rows(us):
            h, r0, n = us[0] // 8, 4 * (us[0] % 8), 4 * len(us)
            nc.sync.dma_start(out=out[32 * h + r0 : 32 * h + r0 + n].rearrange("i j c -> j i c"), in_=xs[h][:, r0 : r0 + n, :])

        for i in range(SCALAR_ROWS, 32):
            normalise(0, i)
        if GP0:
            on_gpsimd(GP0)
        second["fa"] = row_stats(x1, 0)
        second["fb"] = row_stats(x1, 16)
        line = [u for u in range(16) if u not in GP0 and u not in GP1]
        ready = [0]
        turn(line[0])
        turn(line[1])
        gain_and_bias(line[0])
        for s in range(len(line)):
            if s == A_AT:
                second["ra"] = inverse_deviation(second["fa"])
            if s == B_AT:
                second["rb"] = inverse_deviation(second["fb"])
            if s + 2 < len(line) and line[s + 2] >= 8:
                while ready[0] < min(line[s + 2] - 8 + LOOK, 7) + 1:
                    for i in range(4 * ready[0], 4 * ready[0] + 4):
                        normalise(1, i)
                    ready[0] += 1
                    if GP1 and ready[0] == 8:
                        on_gpsimd(GP1)
            if s == GP0_STORE_AT and GP0:
                store_rows(GP0)
            if s + 2 < len(line):
                turn(line[s + 2])
            if s + 1 < len(line):
                gain_and_bias(line[s + 1])
            turn_back_and_store(line[s])
        if GP1:
            store_rows(GP1)
